import numpy as np
import ml_dtypes


def mxq(x, axis, fmt="e4m3"):
    dtype, down = {"e4m3": (ml_dtypes.float8_e4m3fn, 7), "e5m2": (ml_dtypes.float8_e5m2, 14)}[fmt]
    v = np.moveaxis(np.asarray(x, np.float32).astype(ml_dtypes.bfloat16).astype(np.float64), axis, -1)
    blocks = v.reshape(v.shape[:-1] + (-1, 32))
    amax = np.abs(blocks).max(-1, keepdims=True)
    byte = np.maximum(np.where(amax > 0, np.frexp(amax)[1] - 1 + 127, 0) - down, 1)
    scale = np.exp2(byte - 127.0)
    codes = (blocks / scale).astype(np.float32).astype(dtype).astype(np.float64)
    return np.moveaxis((codes * scale).reshape(v.shape), -1, axis)


WIDE = False


def mx_kscale(k):
    if not WIDE:
        return np.ones(k)
    levels = np.array([10, -10, 5, -5, 0])
    a = np.random.permutation(np.resize(levels, k // 512 * 4)).reshape(k // 512, 4)
    idx = np.arange(k)
    return np.exp2(a[idx // 512, idx % 128 // 32])


BF16 = ml_dtypes.bfloat16


def bf(x):
    return np.asarray(x, np.float32).astype(BF16)


def f64(x):
    return np.asarray(x).astype(np.float64)


B, E, LATENT, COND, HIDDEN, OUT, GH = 4096, 4, 256, 768, 256, 256, 128
INPUT = LATENT + COND
EPS = 1e-5


def elu(v):
    return np.where(v > 0.0, v, np.exp(np.minimum(v, 0.0)) - 1.0)


def layernorm(v):
    mu = v.mean(-1, keepdims=True)
    var = np.square(v - mu).mean(-1, keepdims=True)
    return (v - mu) / np.sqrt(var + EPS)


def softmax(v):
    e = np.exp(v - v.max(-1, keepdims=True))
    return e / e.sum(-1, keepdims=True)


def setup_inputs():
    rn = np.random.standard_normal
    swap = np.arange(INPUT) ^ 1
    s = f64(mx_kscale(INPUT))
    s = np.minimum(s, s[swap])
    g = np.exp2(np.round(np.log2(np.sqrt(np.mean(s * s)))))
    u = rn((B, INPUT))
    pair = f64(bf((u - u[:, swap]) * np.sqrt(0.5)))
    gen = np.concatenate([0.5 * rn((B, LATENT)), 0.4 + rn((B, COND))], axis=1)
    x = pair * s + np.min(s) ** 3 * gen
    return {"z": bf(x[:, :LATENT]),
            "c": bf(x[:, LATENT:]),
            "gate_logits": bf(1.5 * rn((B, E))),
            "w0": bf(rn((E, INPUT, HIDDEN)) * 1.5 / np.sqrt(INPUT) / s[None, :, None] * g),
            "b0": bf(rn((E, HIDDEN)) * 0.5)}


def reference(z, c, gate_logits, w0, b0):
    coeff = softmax(f64(gate_logits))
    inp = layernorm(np.concatenate([f64(z), f64(c)], axis=-1))
    y = mxq(inp, 1, "e4m3") @ mxq(f64(w0), 1, "e4m3")
    mixed = (coeff.T[:, :, None] * y).sum(0)
    mixed_bias = (coeff[:, :, None] * f64(b0)[None]).sum(1)
    return elu(mixed + mixed_bias)

@@ -1,0 +1,409 @@
+from contextlib import ExitStack
+
+import concourse.mybir as mybir
+from concourse.masks import make_identity
+
+F32 = mybir.dt.float32
+BF16 = mybir.dt.bfloat16
+U32 = mybir.dt.uint32
+U8 = mybir.dt.uint8
+FP8X4 = mybir.dt.float8_e4m3fn_x4
+ALU = mybir.AluOpType
+ACT = mybir.ActivationFunctionType
+AXIS = mybir.AxisListType
+
+P = 128
+ROWS = 4096
+LATENT = 256
+FEATURES = 1024
+EXPERTS = 4
+HIDDEN = 256
+EPS = 1e-5
+
+TILES = ROWS // P
+PAIR = 2
+PAIRS = TILES // PAIR
+PACK = 4
+K_PASS = P * PACK
+PASSES = FEATURES // K_PASS
+WORDS = FEATURES // PACK
+N_COLS = 512
+HALVES = EXPERTS * HIDDEN // N_COLS
+BN_CHUNK = 512
+HEAD_PAIRS = 5
+HEAD_TILES = HEAD_PAIRS * PAIR
+PIECES = 3
+SLOT = 16
+SLOT_TILES = P // SLOT
+
+FLOPS = 2 * ROWS * FEATURES * EXPERTS * HIDDEN
+
+
+def tile_gatingmixeddecoder_pa_t_kernel(tc, z, c, gate_logits, w0, b0, out):
+    nc = tc.nc
+    z_rows = z.rearrange("(p t) k -> p t k", t=TILES)
+    c_rows = c.rearrange("(p t) k -> p t k", t=TILES)
+    out_rows = out.rearrange("(p t) h -> p t h", t=TILES)
+
+    with ExitStack() as ctx:
+        keep = ctx.enter_context(tc.tile_pool(name="keep", bufs=1))
+        stage = ctx.enter_context(tc.tile_pool(name="stage", bufs=2))
+        flow = ctx.enter_context(tc.tile_pool(name="flow", bufs=3))
+        small = ctx.enter_context(tc.tile_pool(name="small", bufs=12))
+        psum_head = ctx.enter_context(tc.psum_pool(name="psum_head", bufs=1))
+        psum_xt = ctx.enter_context(tc.psum_pool(name="psum_xt", bufs=2))
+        psum_y = ctx.enter_context(tc.psum_pool(name="psum_y", bufs=2))
+        psum_bias = ctx.enter_context(tc.psum_pool(name="psum_bias", bufs=1))
+        ctx.enter_context(tc.manual_schedule())
+
+        gate = keep.tile([P, TILES, EXPERTS], BF16)
+        nc.sync.dma_start(out=gate[:], in_=gate_logits.rearrange("(p t) e -> p t e", t=TILES))
+
+        bias_rows = keep.tile([P, HIDDEN], BF16)
+        nc.vector.memset(bias_rows[:], 0.0)
+        nc.sync.dma_start(out=bias_rows[0:EXPERTS, :], in_=b0)
+
+        x_pairs = [
+            keep.tile([P, PAIR, FEATURES], BF16, name="x_pair%d" % q) for q in range(PAIRS)
+        ]
+
+        def load_pair(q):
+            tiles = slice(q * PAIR, (q + 1) * PAIR)
+            nc.sync.dma_start(out=x_pairs[q][:, :, 0:LATENT], in_=z_rows[:, tiles, :])
+            nc.sync.dma_start(out=x_pairs[q][:, :, LATENT:FEATURES], in_=c_rows[:, tiles, :])
+
+        w_raw = keep.tile([P, EXPERTS, PASSES * 2, 2 * HIDDEN], BF16)
+
+        for q in range(2):
+            load_pair(q)
+            load_pair(HEAD_PAIRS + q)
+        for x in range(EXPERTS):
+            nc.sync.dma_start(
+                out=w_raw[:, x, :, :],
+                in_=w0[x].rearrange("(gu p e) h -> p gu (e h)", p=P, e=2),
+            )
+        for q in range(2, HEAD_PAIRS):
+            load_pair(q)
+            load_pair(HEAD_PAIRS + q)
+        for q in range(2 * HEAD_PAIRS, PAIRS):
+            load_pair(q)
+
+        ident_f32 = keep.tile([P, P], F32)
+        make_identity(nc, ident_f32[:])
+        ident_bf16 = keep.tile([P, P], BF16)
+        make_identity(nc, ident_bf16[:])
+        neg_half = keep.tile([P, 1], F32)
+        nc.vector.memset(neg_half[:], -0.5)
+
+        wide = [P, TILES, EXPERTS]
+        gate_max = keep.tile([P, TILES], F32)
+        nc.vector.tensor_reduce(out=gate_max[:], in_=gate[:], axis=AXIS.X, op=ALU.max)
+        gate_exp = keep.tile(wide, F32)
+        nc.vector.tensor_tensor(
+            out=gate_exp[:], in0=gate[:], in1=gate_max[:].unsqueeze(2).to_broadcast(wide),
+            op=ALU.subtract,
+        )
+        nc.scalar.activation(out=gate_exp[:], in_=gate_exp[:], func=ACT.Exp)
+        coeff = keep.tile(wide, F32)
+        pieces = keep.tile([P, TILES, SLOT], BF16)
+        blocks = TILES // SLOT_TILES
+        pieces_ps = psum_head.tile([P, blocks, P], BF16)
+        pieces_t = keep.tile([P, blocks, P], BF16)
+        spread = keep.tile([P, P // EXPERTS, EXPERTS], BF16)
+        bias_ps = psum_bias.tile([P, HIDDEN], F32, tag="bias")
+        bias_all = keep.tile([P, HIDDEN], BF16)
+        in_slot = keep.tile([P, SLOT_TILES], F32)
+        bias_slot = keep.tile([P, SLOT_TILES, HIDDEN], BF16)
+
+        def finish_coefficients():
+            gate_sum = keep.tile([P, TILES], F32)
+            nc.vector.tensor_reduce(out=gate_sum[:], in_=gate_exp[:], axis=AXIS.X, op=ALU.add)
+            gate_inv = keep.tile([P, TILES], F32)
+            nc.vector.reciprocal(out=gate_inv[:], in_=gate_sum[:])
+            nc.vector.tensor_tensor(
+                out=coeff[:], in0=gate_exp[:], in1=gate_inv[:].unsqueeze(2).to_broadcast(wide),
+                op=ALU.mult,
+            )
+
+        def start_bias_operands():
+            nc.vector.memset(pieces[:], 0.0)
+            rest = coeff
+            for i in range(PIECES):
+                piece = pieces[:, :, i * EXPERTS : (i + 1) * EXPERTS]
+                nc.vector.tensor_copy(out=piece, in_=rest[:])
+                if i < PIECES - 1:
+                    next_rest = keep.tile(wide, F32, name="rest%d" % i)
+                    nc.vector.tensor_tensor(
+                        out=next_rest[:], in0=rest[:], in1=piece, op=ALU.subtract
+                    )
+                    rest = next_rest
+            for a in range(blocks):
+                nc.tensor.transpose(
+                    pieces_ps[:, a, :],
+                    pieces[:, a * SLOT_TILES : (a + 1) * SLOT_TILES, :].rearrange(
+                        "p b j -> p (b j)"
+                    ),
+                    ident_bf16[:],
+                )
+            nc.vector.tensor_copy(
+                out=spread[:],
+                in_=ident_bf16[:, 0:EXPERTS].unsqueeze(1).to_broadcast(
+                    [P, P // EXPERTS, EXPERTS]
+                ),
+            )
+            nc.tensor.matmul(
+                out=bias_ps[:], lhsT=spread[:].rearrange("p a e -> p (a e)"), rhs=bias_rows[:],
+                start=True, stop=True,
+            )
+            nc.vector.tensor_reduce(
+                out=in_slot[:], in_=ident_f32[:].rearrange("p (b j) -> p b j", j=SLOT),
+                axis=AXIS.X, op=ALU.add,
+            )
+
+        def finish_bias_operands():
+            nc.vector.tensor_copy(out=pieces_t[:], in_=pieces_ps[:])
+            nc.vector.tensor_copy(out=bias_all[:], in_=bias_ps[:])
+            for b in range(SLOT_TILES):
+                nc.vector.tensor_scalar(
+                    out=bias_slot[:, b, :], in0=bias_all[:], scalar1=in_slot[:, b : b + 1],
+                    scalar2=None, op0=ALU.mult,
+                )
+
+        w_codes = keep.tile([P, PASSES, EXPERTS * HIDDEN], U32, align_bytes=64)
+        w_scales = keep.tile([P, PASSES, EXPERTS * HIDDEN], U8, align_bytes=64)
+
+        per_half = EXPERTS // HALVES
+        w_grouped = {}
+
+        def regroup_weights():
+            for half in range(HALVES):
+                for g in range(PASSES):
+                    w_grouped[g, half] = keep.tile(
+                        [P, per_half, HIDDEN, PACK], BF16, name="w_grouped%d%d" % (g, half),
+                        align_bytes=64,
+                    )
+                    for i in range(per_half):
+                        planes = w_raw[:, half * per_half + i, 2 * g : 2 * g + 2, :].rearrange(
+                            "p u (e h) -> p (u e) h", e=2
+                        )
+                        source = planes.rearrange("p j (n i) -> p n j i", i=4)
+                        target = w_grouped[g, half][:, i, :, :].rearrange(
+                            "p (n i) j -> p n j i", i=4
+                        )
+                        if i % 2 == 0:
+                            nc.vector.tensor_copy(out=target, in_=source)
+                        else:
+                            nc.scalar.copy(out=target, in_=source)
+
+        def quantise_weights():
+            for half in range(HALVES):
+                for g in range(PASSES):
+                    cols = slice(half * N_COLS, (half + 1) * N_COLS)
+                    nc.vector.quantize_mx(
+                        out=w_codes[:, g, cols].bitcast(FP8X4),
+                        scales=w_scales[:, g, cols],
+                        in_=w_grouped[g, half][:].rearrange("p x h j -> p (x h j)"),
+                    )
+
+        shift = {}
+        rstd = {}
+        normed = {}
+        turned = {}
+        grouped = {}
+        codes = {}
+        products = {}
+        bias_mix = {}
+        mixed = {}
+        mixed_exp = {}
+
+        def inverse_std(t, spread_sum, scale):
+            var_eps = small.tile([P, 1], F32)
+            nc.gpsimd.tensor_scalar(
+                out=var_eps[:], in0=spread_sum, scalar1=scale, scalar2=EPS,
+                op0=ALU.mult, op1=ALU.add,
+            )
+            rstd[t] = keep.tile([P, 1], F32, name="rstd%d" % t)
+            nc.gpsimd.tensor_tensor(out=rstd[t][:], in0=var_eps[:], in1=neg_half[:], op=ALU.pow)
+
+        def x_tile(t):
+            return x_pairs[t // PAIR][:, t % PAIR, :]
+
+        def vector_stats(q):
+            for t in range(q * PAIR, (q + 1) * PAIR):
+                chunks = small.tile([P, FEATURES // BN_CHUNK, 6], F32)
+                for n in range(FEATURES // BN_CHUNK):
+                    nc.vector.bn_stats(
+                        out=chunks[:, n, :], in_=x_tile(t)[:, n * BN_CHUNK : (n + 1) * BN_CHUNK]
+                    )
+                mean_var = small.tile([P, 2], F32)
+                nc.vector.bn_aggr(out=mean_var[:], in_=chunks[:].rearrange("p n s -> p (n s)"))
+                inverse_std(t, mean_var[:, 1:2], 1.0)
+                chunk_means = small.tile([P, FEATURES // BN_CHUNK], F32)
+                nc.gpsimd.tensor_tensor(
+                    out=chunk_means[:], in0=chunks[:, :, 1], in1=chunks[:, :, 4], op=ALU.add
+                )
+                means_sum = small.tile([P, 1], F32)
+                nc.gpsimd.tensor_tensor(
+                    out=means_sum[:], in0=chunk_means[:, 0:1], in1=chunk_means[:, 1:2], op=ALU.add
+                )
+                neg_mean = keep.tile([P, 1], F32, name="neg_mean%d" % t)
+                nc.gpsimd.tensor_scalar(
+                    out=neg_mean[:], in0=means_sum[:], scalar1=-0.25, scalar2=0.0,
+                    op0=ALU.mult, op1=ALU.add,
+                )
+                shift[t] = (neg_mean, ALU.add)
+
+        def scalar_mean(t):
+            unread = stage.tile([P, FEATURES], BF16, name="unread_sum")
+            total = small.tile([P, 1], F32)
+            nc.scalar.activation(
+                out=unread[:], in_=x_tile(t), func=ACT.Identity, accum_out=total[:]
+            )
+            neg_mean = keep.tile([P, 1], F32, name="neg_mean%d" % t)
+            nc.gpsimd.tensor_scalar(
+                out=neg_mean[:], in0=total[:], scalar1=-1.0 / FEATURES, scalar2=0.0,
+                op0=ALU.mult, op1=ALU.add,
+            )
+            shift[t] = (neg_mean, ALU.add)
+
+        def scalar_spread(t):
+            unread = stage.tile([P, FEATURES], BF16, name="unread_square")
+            squares = small.tile([P, 1], F32)
+            nc.scalar.activation(
+                out=unread[:], in_=x_tile(t), func=ACT.Square, bias=shift[t][0][:],
+                scale=1.0, accum_out=squares[:],
+            )
+            inverse_std(t, squares[:], 1.0 / FEATURES)
+
+        def normalise(q):
+            normed[q] = stage.tile([P, PAIR, FEATURES], BF16, name="normed")
+            for i in range(PAIR):
+                t = q * PAIR + i
+                nc.vector.tensor_scalar(
+                    out=normed[q][:, i, :], in0=x_pairs[q][:, i, :],
+                    scalar1=shift[t][0][:], scalar2=rstd[t][:], op0=shift[t][1], op1=ALU.mult,
+                )
+
+        def transpose(q):
+            turned[q] = []
+            for i in range(PAIR):
+                words = normed[q][:, i, :].bitcast(F32)
+                planes = psum_xt.tile([P, PASSES, 2, P], F32)
+                for g in range(PASSES):
+                    for u in range(2):
+                        first = (2 * g + u) * P
+                        nc.tensor.transpose(
+                            planes[:, g, u, :], words[:, first : first + P], ident_f32[:]
+                        )
+                turned[q].append(planes)
+
+        def regroup(q):
+            grouped[q] = stage.tile([P, PAIR, FEATURES], BF16, name="grouped", align_bytes=64)
+            for i in range(PAIR):
+                nc.scalar.copy(
+                    out=grouped[q][:, i, :].bitcast(F32).rearrange(
+                        "p (g r u) -> p g r u", g=PASSES, u=2
+                    ),
+                    in_=turned[q][i][:].rearrange("p g u r -> p g r u"),
+                )
+
+        def quantise(q):
+            words = flow.tile([P, PAIR * WORDS], U32, name="a_codes", align_bytes=64)
+            plane = flow.tile([P, PAIR * WORDS], U8, name="a_scales", align_bytes=64)
+            nc.vector.quantize_mx(
+                out=words[:].bitcast(FP8X4), scales=plane[:],
+                in_=grouped[q][:].rearrange("p i k -> p (i k)"),
+            )
+            codes[q] = (words, plane)
+
+        def bias_product(q):
+            both = psum_bias.tile([P, PAIR, HIDDEN], F32, tag="bias")
+            for i in range(PAIR):
+                t = q * PAIR + i
+                nc.tensor.matmul(
+                    out=both[:, i, :], lhsT=pieces_t[:, t // SLOT_TILES, :],
+                    rhs=bias_slot[:, t % SLOT_TILES, :], start=True, stop=True,
+                )
+            bias_mix[q] = flow.tile([P, PAIR, HIDDEN], F32, name="bias_mix")
+            nc.scalar.copy(out=bias_mix[q][:], in_=both[:])
+
+        def multiply(q):
+            words, plane = codes[q]
+            products[q] = [[], []]
+            for half in range(HALVES):
+                cols = slice(half * N_COLS, (half + 1) * N_COLS)
+                for i in range(PAIR):
+                    bank = psum_y.tile([P, N_COLS], F32, name="y%d" % half)
+                    for g in range(PASSES):
+                        rows = slice(i * WORDS + g * P, i * WORDS + (g + 1) * P)
+                        nc.tensor.matmul_mx(
+                            out=bank[:],
+                            lhsT=words[:, rows].bitcast(FP8X4), lhsT_scale=plane[:, rows],
+                            rhs=w_codes[:, g, cols].bitcast(FP8X4), rhs_scale=w_scales[:, g, cols],
+                            start=(g == 0), stop=(g == PASSES - 1),
+                        )
+                    products[q][i].append(bank)
+
+        def mix(q):
+            mixed[q] = flow.tile([P, PAIR, HIDDEN], F32, name="mixed")
+            for x in range(EXPERTS):
+                for i in range(PAIR):
+                    t = q * PAIR + i
+                    bank = products[q][i][x * HIDDEN // N_COLS]
+                    first = x * HIDDEN % N_COLS
+                    nc.vector.scalar_tensor_tensor(
+                        out=mixed[q][:, i, :], in0=bank[:, first : first + HIDDEN],
+                        scalar=coeff[:, t, x : x + 1],
+                        in1=(bias_mix[q] if x == 0 else mixed[q])[:, i, :],
+                        op0=ALU.mult, op1=ALU.add,
+                    )
+
+        def exponential(q):
+            mixed_exp[q] = flow.tile([P, PAIR, HIDDEN], F32, name="mixed_exp")
+            nc.scalar.activation(out=mixed_exp[q][:], in_=mixed[q][:], func=ACT.Exp)
+
+        def elu_and_store(q):
+            below = flow.tile([P, PAIR, HIDDEN], F32)
+            nc.vector.tensor_scalar(
+                out=below[:], in0=mixed_exp[q][:], scalar1=1.0, scalar2=-1.0,
+                op0=ALU.min, op1=ALU.add,
+            )
+            result = flow.tile([P, PAIR, HIDDEN], F32)
+            nc.vector.tensor_tensor(out=result[:], in0=mixed[q][:], in1=below[:], op=ALU.max)
+            nc.sync.dma_start(out=out_rows[:, q * PAIR : (q + 1) * PAIR, :], in_=result[:])
+
+        def run(stage_of_pair, q, last=PAIRS):
+            if 0 <= q < last:
+                stage_of_pair(q)
+
+        def scalar_stats(n):
+            if HEAD_TILES + n + 1 < TILES:
+                scalar_mean(HEAD_TILES + n + 1)
+            if HEAD_TILES + n < TILES:
+                scalar_spread(HEAD_TILES + n)
+
+        scalar_mean(HEAD_TILES)
+        for s in range(-4, PAIRS + 1):
+            run(exponential, s - 1)
+            if s == -2:
+                finish_coefficients()
+                start_bias_operands()
+            run(normalise, s + 2)
+            run(transpose, s + 2)
+            if s == -2:
+                regroup_weights()
+                finish_bias_operands()
+            if s == -1:
+                quantise_weights()
+            run(quantise, s + 1)
+            run(bias_product, s + 1)
+            run(mix, s)
+            run(multiply, s + 1)
+            run(elu_and_store, s - 1)
+            run(vector_stats, s + 4, HEAD_PAIRS)
+            run(regroup, s + 2)
+            if s + 4 < HEAD_PAIRS:
+                scalar_stats(PAIR * (s + 4))
+                scalar_stats(PAIR * (s + 4) + 1)
+            else:
+                scalar_stats(HEAD_PAIRS + s + 4)

@@ -92,7 +92,7 @@ def tile_gatingmixeddecoder_pa_t_kernel(tc, z, c, gate_logits, w0, b0, out):
         make_identity(nc, ident_f32[:])
         ident_bf16 = keep.tile([P, P], BF16)
         make_identity(nc, ident_bf16[:])
-        neg_half = keep.tile([P, 1], F32)
+        neg_half = keep.tile([P, PAIR], F32)
         nc.vector.memset(neg_half[:], -0.5)
 
         wide = [P, TILES, EXPERTS]
@@ -205,8 +205,6 @@ def tile_gatingmixeddecoder_pa_t_kernel(tc, z, c, gate_logits, w0, b0, out):
                         in_=w_grouped[g, half][:].rearrange("p x h j -> p (x h j)"),
                     )
 
-        shift = {}
-        rstd = {}
         normed = {}
         turned = {}
         grouped = {}
@@ -216,72 +214,74 @@ def tile_gatingmixeddecoder_pa_t_kernel(tc, z, c, gate_logits, w0, b0, out):
         mixed = {}
         mixed_exp = {}
 
-        def inverse_std(t, spread_sum, scale):
-            var_eps = small.tile([P, 1], F32)
-            nc.gpsimd.tensor_scalar(
-                out=var_eps[:], in0=spread_sum, scalar1=scale, scalar2=EPS,
-                op0=ALU.mult, op1=ALU.add,
-            )
-            rstd[t] = keep.tile([P, 1], F32, name="rstd%d" % t)
-            nc.gpsimd.tensor_tensor(out=rstd[t][:], in0=var_eps[:], in1=neg_half[:], op=ALU.pow)
-
         def x_tile(t):
             return x_pairs[t // PAIR][:, t % PAIR, :]
 
+        mean = [keep.tile([P, PAIR], F32, name="mean%d" % q) for q in range(PAIRS)]
+        rstd = [keep.tile([P, PAIR], F32, name="rstd%d" % q) for q in range(PAIRS)]
+        squares = {}
+
+        def inverse_std(q, spread, scale):
+            var_eps = small.tile([P, PAIR], F32)
+            nc.gpsimd.tensor_scalar(
+                out=var_eps[:], in0=spread, scalar1=scale, scalar2=EPS,
+                op0=ALU.mult, op1=ALU.add,
+            )
+            nc.gpsimd.tensor_tensor(
+                out=rstd[q][:], in0=var_eps[:], in1=neg_half[:], op=ALU.pow
+            )
+
         def vector_stats(q):
-            for t in range(q * PAIR, (q + 1) * PAIR):
-                chunks = small.tile([P, FEATURES // BN_CHUNK, 6], F32)
+            chunks = small.tile([P, PAIR, FEATURES // BN_CHUNK, 6], F32)
+            mean_var = small.tile([P, PAIR, 2], F32)
+            for i in range(PAIR):
                 for n in range(FEATURES // BN_CHUNK):
                     nc.vector.bn_stats(
-                        out=chunks[:, n, :], in_=x_tile(t)[:, n * BN_CHUNK : (n + 1) * BN_CHUNK]
+                        out=chunks[:, i, n, :],
+                        in_=x_pairs[q][:, i, n * BN_CHUNK : (n + 1) * BN_CHUNK],
                     )
-                mean_var = small.tile([P, 2], F32)
-                nc.vector.bn_aggr(out=mean_var[:], in_=chunks[:].rearrange("p n s -> p (n s)"))
-                inverse_std(t, mean_var[:, 1:2], 1.0)
-                chunk_means = small.tile([P, FEATURES // BN_CHUNK], F32)
-                nc.gpsimd.tensor_tensor(
-                    out=chunk_means[:], in0=chunks[:, :, 1], in1=chunks[:, :, 4], op=ALU.add
+            for i in range(PAIR):
+                nc.vector.bn_aggr(
+                    out=mean_var[:, i, :], in_=chunks[:, i, :, :].rearrange("p n s -> p (n s)")
                 )
-                means_sum = small.tile([P, 1], F32)
-                nc.gpsimd.tensor_tensor(
-                    out=means_sum[:], in0=chunk_means[:, 0:1], in1=chunk_means[:, 1:2], op=ALU.add
-                )
-                neg_mean = keep.tile([P, 1], F32, name="neg_mean%d" % t)
-                nc.gpsimd.tensor_scalar(
-                    out=neg_mean[:], in0=means_sum[:], scalar1=-0.25, scalar2=0.0,
-                    op0=ALU.mult, op1=ALU.add,
-                )
-                shift[t] = (neg_mean, ALU.add)
+            means_sum = small.tile([P, PAIR], F32)
+            nc.vector.tensor_reduce(
+                out=means_sum[:],
+                in_=chunks[:].rearrange("p i n (a s) -> p i (n a) s", a=2)[:, :, :, 1],
+                axis=AXIS.X, op=ALU.add,
+            )
+            nc.gpsimd.tensor_scalar(
+                out=mean[q][:], in0=means_sum[:], scalar1=BN_CHUNK / (2.0 * FEATURES),
+                scalar2=0.0, op0=ALU.mult, op1=ALU.add,
+            )
+            inverse_std(q, mean_var[:, :, 1], 1.0)
 
         def scalar_mean(t):
             unread = stage.tile([P, FEATURES], BF16, name="unread_sum")
-            total = small.tile([P, 1], F32)
             nc.scalar.activation(
-                out=unread[:], in_=x_tile(t), func=ACT.Identity, accum_out=total[:]
+                out=unread[:], in_=x_tile(t), func=ACT.Identity, scale=1.0 / FEATURES,
+                accum_out=mean[t // PAIR][:, t % PAIR : t % PAIR + 1],
             )
-            neg_mean = keep.tile([P, 1], F32, name="neg_mean%d" % t)
-            nc.gpsimd.tensor_scalar(
-                out=neg_mean[:], in0=total[:], scalar1=-1.0 / FEATURES, scalar2=0.0,
-                op0=ALU.mult, op1=ALU.add,
-            )
-            shift[t] = (neg_mean, ALU.add)
 
         def scalar_spread(t):
+            q, i = t // PAIR, t % PAIR
             unread = stage.tile([P, FEATURES], BF16, name="unread_square")
-            squares = small.tile([P, 1], F32)
+            if i == 0:
+                squares[q] = small.tile([P, PAIR], F32, name="squares")
             nc.scalar.activation(
-                out=unread[:], in_=x_tile(t), func=ACT.Square, bias=shift[t][0][:],
-                scale=1.0, accum_out=squares[:],
+                out=unread[:], in_=x_tile(t), func=ACT.Square, bias=mean[q][:, i : i + 1],
+                scale=-1.0, accum_out=squares[q][:, i : i + 1],
             )
-            inverse_std(t, squares[:], 1.0 / FEATURES)
+            if i == PAIR - 1:
+                inverse_std(q, squares[q][:], 1.0 / FEATURES)
 
         def normalise(q):
             normed[q] = stage.tile([P, PAIR, FEATURES], BF16, name="normed")
             for i in range(PAIR):
-                t = q * PAIR + i
                 nc.vector.tensor_scalar(
                     out=normed[q][:, i, :], in0=x_pairs[q][:, i, :],
-                    scalar1=shift[t][0][:], scalar2=rstd[t][:], op0=shift[t][1], op1=ALU.mult,
+                    scalar1=mean[q][:, i : i + 1], scalar2=rstd[q][:, i : i + 1],
+                    op0=ALU.subtract, op1=ALU.mult,
                 )
 
         def transpose(q):

@@ -30,8 +30,11 @@ WORDS = FEATURES // PACK
 N_COLS = 512
 HALVES = EXPERTS * HIDDEN // N_COLS
 BN_CHUNK = 512
-HEAD_PAIRS = 5
-HEAD_TILES = HEAD_PAIRS * PAIR
+HEAD_PAIRS = 3
+GROUP = 2
+SUMMED_FIRST = HEAD_PAIRS + GROUP
+SUMMED_PAIRS = 4 * GROUP
+SUMMED_LAST = SUMMED_FIRST + SUMMED_PAIRS
 PIECES = 3
 SLOT = 16
 SLOT_TILES = P // SLOT
@@ -48,20 +51,20 @@ def tile_gatingmixeddecoder_pa_t_kernel(tc, z, c, gate_logits, w0, b0, out):
     with ExitStack() as ctx:
         keep = ctx.enter_context(tc.tile_pool(name="keep", bufs=1))
         stage = ctx.enter_context(tc.tile_pool(name="stage", bufs=2))
-        flow = ctx.enter_context(tc.tile_pool(name="flow", bufs=3))
+        flow = ctx.enter_context(tc.tile_pool(name="flow", bufs=4))
         small = ctx.enter_context(tc.tile_pool(name="small", bufs=12))
-        psum_head = ctx.enter_context(tc.psum_pool(name="psum_head", bufs=1))
+        psum_sum = ctx.enter_context(tc.psum_pool(name="psum_sum", bufs=1))
         psum_xt = ctx.enter_context(tc.psum_pool(name="psum_xt", bufs=2))
         psum_y = ctx.enter_context(tc.psum_pool(name="psum_y", bufs=2))
         psum_bias = ctx.enter_context(tc.psum_pool(name="psum_bias", bufs=1))
         ctx.enter_context(tc.manual_schedule())
 
         gate = keep.tile([P, TILES, EXPERTS], BF16)
-        nc.sync.dma_start(out=gate[:], in_=gate_logits.rearrange("(p t) e -> p t e", t=TILES))
+        nc.scalar.dma_start(out=gate[:], in_=gate_logits.rearrange("(p t) e -> p t e", t=TILES))
 
         bias_rows = keep.tile([P, HIDDEN], BF16)
         nc.vector.memset(bias_rows[:], 0.0)
-        nc.sync.dma_start(out=bias_rows[0:EXPERTS, :], in_=b0)
+        nc.scalar.dma_start(out=bias_rows[0:EXPERTS, :], in_=b0)
 
         x_pairs = [
             keep.tile([P, PAIR, FEATURES], BF16, name="x_pair%d" % q) for q in range(PAIRS)
@@ -92,8 +95,15 @@ def tile_gatingmixeddecoder_pa_t_kernel(tc, z, c, gate_logits, w0, b0, out):
         make_identity(nc, ident_f32[:])
         ident_bf16 = keep.tile([P, P], BF16)
         make_identity(nc, ident_bf16[:])
-        neg_half = keep.tile([P, PAIR], F32)
+        ident_mean = keep.tile([P, P], BF16)
+        nc.vector.tensor_scalar(
+            out=ident_mean[:], in0=ident_bf16[:], scalar1=1.0 / FEATURES, scalar2=None,
+            op0=ALU.mult,
+        )
+        neg_half = keep.tile([P, GROUP * PAIR], F32)
         nc.vector.memset(neg_half[:], -0.5)
+        eps = keep.tile([P, 1], F32)
+        nc.vector.memset(eps[:], EPS)
 
         wide = [P, TILES, EXPERTS]
         gate_max = keep.tile([P, TILES], F32)
@@ -107,7 +117,7 @@ def tile_gatingmixeddecoder_pa_t_kernel(tc, z, c, gate_logits, w0, b0, out):
         coeff = keep.tile(wide, F32)
         pieces = keep.tile([P, TILES, SLOT], BF16)
         blocks = TILES // SLOT_TILES
-        pieces_ps = psum_head.tile([P, blocks, P], BF16)
+        pieces_ps = psum_sum.tile([P, blocks, P], BF16, tag="sum")
         pieces_t = keep.tile([P, blocks, P], BF16)
         spread = keep.tile([P, P // EXPERTS, EXPERTS], BF16)
         bias_ps = psum_bias.tile([P, HIDDEN], F32, tag="bias")
@@ -115,28 +125,38 @@ def tile_gatingmixeddecoder_pa_t_kernel(tc, z, c, gate_logits, w0, b0, out):
         in_slot = keep.tile([P, SLOT_TILES], F32)
         bias_slot = keep.tile([P, SLOT_TILES, HIDDEN], BF16)
 
-        def finish_coefficients():
-            gate_sum = keep.tile([P, TILES], F32)
-            nc.vector.tensor_reduce(out=gate_sum[:], in_=gate_exp[:], axis=AXIS.X, op=ALU.add)
-            gate_inv = keep.tile([P, TILES], F32)
-            nc.vector.reciprocal(out=gate_inv[:], in_=gate_sum[:])
-            nc.vector.tensor_tensor(
+        gate_sum = keep.tile([P, TILES], F32)
+        gate_inv = keep.tile([P, TILES], F32)
+        rests = [coeff]
+        for i in range(PIECES - 1):
+            rests.append(keep.tile(wide, F32, name="rest%d" % i))
+
+        def piece(i):
+            return pieces[:, :, i * EXPERTS : (i + 1) * EXPERTS]
+
+        coefficient_steps = [
+            lambda: nc.vector.tensor_reduce(
+                out=gate_sum[:], in_=gate_exp[:], axis=AXIS.X, op=ALU.add
+            ),
+            lambda: nc.vector.reciprocal(out=gate_inv[:], in_=gate_sum[:]),
+            lambda: nc.vector.tensor_tensor(
                 out=coeff[:], in0=gate_exp[:], in1=gate_inv[:].unsqueeze(2).to_broadcast(wide),
                 op=ALU.mult,
+            ),
+            lambda: nc.vector.memset(pieces[:], 0.0),
+        ]
+        for i in range(PIECES):
+            coefficient_steps.append(
+                lambda i=i: nc.vector.tensor_copy(out=piece(i), in_=rests[i][:])
             )
+            if i < PIECES - 1:
+                coefficient_steps.append(
+                    lambda i=i: nc.vector.tensor_tensor(
+                        out=rests[i + 1][:], in0=rests[i][:], in1=piece(i), op=ALU.subtract
+                    )
+                )
 
         def start_bias_operands():
-            nc.vector.memset(pieces[:], 0.0)
-            rest = coeff
-            for i in range(PIECES):
-                piece = pieces[:, :, i * EXPERTS : (i + 1) * EXPERTS]
-                nc.vector.tensor_copy(out=piece, in_=rest[:])
-                if i < PIECES - 1:
-                    next_rest = keep.tile(wide, F32, name="rest%d" % i)
-                    nc.vector.tensor_tensor(
-                        out=next_rest[:], in0=rest[:], in1=piece, op=ALU.subtract
-                    )
-                    rest = next_rest
             for a in range(blocks):
                 nc.tensor.transpose(
                     pieces_ps[:, a, :],
@@ -213,74 +233,124 @@ def tile_gatingmixeddecoder_pa_t_kernel(tc, z, c, gate_logits, w0, b0, out):
         bias_mix = {}
         mixed = {}
         mixed_exp = {}
+        below = {}
 
         def x_tile(t):
             return x_pairs[t // PAIR][:, t % PAIR, :]
 
-        mean = [keep.tile([P, PAIR], F32, name="mean%d" % q) for q in range(PAIRS)]
-        rstd = [keep.tile([P, PAIR], F32, name="rstd%d" % q) for q in range(PAIRS)]
-        squares = {}
+        group = {}
+        mean = {}
+        rstd = {}
+        sums = {}
+        spreads = {}
+        chunks = {}
+        for first, last in ((0, HEAD_PAIRS), (HEAD_PAIRS, PAIRS)):
+            for start in range(first, last, GROUP):
+                members = range(start, min(start + GROUP, last))
+                columns = len(members) * PAIR
+                group_mean = keep.tile([P, columns], F32, name="mean%d" % start)
+                group_rstd = keep.tile([P, columns], F32, name="rstd%d" % start)
+                for q in members:
+                    group[q], mean[q], rstd[q] = members, group_mean, group_rstd
 
-        def inverse_std(q, spread, scale):
-            var_eps = small.tile([P, PAIR], F32)
-            nc.gpsimd.tensor_scalar(
-                out=var_eps[:], in0=spread, scalar1=scale, scalar2=EPS,
-                op0=ALU.mult, op1=ALU.add,
-            )
+        def column(q, i):
+            return slice((q - group[q].start) * PAIR + i, (q - group[q].start) * PAIR + i + 1)
+
+        def inverse_std(q, var_eps):
             nc.gpsimd.tensor_tensor(
-                out=rstd[q][:], in0=var_eps[:], in1=neg_half[:], op=ALU.pow
+                out=rstd[q][:], in0=var_eps[:], in1=neg_half[:, 0 : len(group[q]) * PAIR],
+                op=ALU.pow,
             )
 
-        def vector_stats(q):
-            chunks = small.tile([P, PAIR, FEATURES // BN_CHUNK, 6], F32)
-            mean_var = small.tile([P, PAIR, 2], F32)
+        def vector_stats(q, between):
+            per_tile = FEATURES // BN_CHUNK
+            columns = len(group[q]) * PAIR
+            if q == group[q].start:
+                chunks[q] = small.tile([P, columns, per_tile, 6], F32, name="chunks")
+            else:
+                chunks[q] = chunks[q - 1]
             for i in range(PAIR):
-                for n in range(FEATURES // BN_CHUNK):
+                for n in range(per_tile):
                     nc.vector.bn_stats(
-                        out=chunks[:, i, n, :],
+                        out=chunks[q][:, column(q, i).start, n, :],
                         in_=x_pairs[q][:, i, n * BN_CHUNK : (n + 1) * BN_CHUNK],
                     )
-            for i in range(PAIR):
-                nc.vector.bn_aggr(
-                    out=mean_var[:, i, :], in_=chunks[:, i, :, :].rearrange("p n s -> p (n s)")
+                    if between:
+                        between[0]()
+                        between.remove(between[0])
+            if q == group[q].stop - 1:
+                mean_var = small.tile([P, columns, 2], F32)
+                for t in range(columns):
+                    nc.vector.bn_aggr(
+                        out=mean_var[:, t, :], in_=chunks[q][:, t, :, :].rearrange("p n s -> p (n s)")
+                    )
+                means_sum = small.tile([P, columns], F32)
+                nc.vector.tensor_reduce(
+                    out=means_sum[:],
+                    in_=chunks[q][:].rearrange("p i n (a s) -> p i (n a) s", a=2)[:, :, :, 1],
+                    axis=AXIS.X, op=ALU.add,
                 )
-            means_sum = small.tile([P, PAIR], F32)
-            nc.vector.tensor_reduce(
-                out=means_sum[:],
-                in_=chunks[:].rearrange("p i n (a s) -> p i (n a) s", a=2)[:, :, :, 1],
-                axis=AXIS.X, op=ALU.add,
-            )
-            nc.gpsimd.tensor_scalar(
-                out=mean[q][:], in0=means_sum[:], scalar1=BN_CHUNK / (2.0 * FEATURES),
-                scalar2=0.0, op0=ALU.mult, op1=ALU.add,
-            )
-            inverse_std(q, mean_var[:, :, 1], 1.0)
+                var_eps = small.tile([P, columns], F32)
+                nc.vector.tensor_scalar(
+                    out=var_eps[:], in0=mean_var[:, :, 1], scalar1=EPS, scalar2=None, op0=ALU.add
+                )
+                nc.vector.tensor_scalar(
+                    out=mean[q][:], in0=means_sum[:], scalar1=1.0 / (2 * per_tile), scalar2=None,
+                    op0=ALU.mult,
+                )
+                inverse_std(q, var_eps)
 
         def scalar_mean(t):
+            q, i = t // PAIR, t % PAIR
             unread = stage.tile([P, FEATURES], BF16, name="unread_sum")
             nc.scalar.activation(
                 out=unread[:], in_=x_tile(t), func=ACT.Identity, scale=1.0 / FEATURES,
-                accum_out=mean[t // PAIR][:, t % PAIR : t % PAIR + 1],
+                accum_out=mean[q][:, column(q, i)],
             )
 
         def scalar_spread(t):
             q, i = t // PAIR, t % PAIR
             unread = stage.tile([P, FEATURES], BF16, name="unread_square")
             if i == 0:
-                squares[q] = small.tile([P, PAIR], F32, name="squares")
+                if q == group[q].start:
+                    spreads[q] = small.tile([P, len(group[q]) * PAIR], F32, name="spreads")
+                else:
+                    spreads[q] = spreads[q - 1]
             nc.scalar.activation(
-                out=unread[:], in_=x_tile(t), func=ACT.Square, bias=mean[q][:, i : i + 1],
-                scale=-1.0, accum_out=squares[q][:, i : i + 1],
+                out=unread[:], in_=x_tile(t), func=ACT.Square, bias=mean[q][:, column(q, i)],
+                scale=-1.0, accum_out=spreads[q][:, column(q, i)],
             )
-            if i == PAIR - 1:
-                inverse_std(q, squares[q][:], 1.0 / FEATURES)
+            if t == group[q].stop * PAIR - 1:
+                var_eps = small.tile([P, len(group[q]) * PAIR], F32)
+                nc.scalar.activation(
+                    out=var_eps[:], in_=spreads[q][:], func=ACT.Identity, bias=eps[:],
+                    scale=1.0 / FEATURES,
+                )
+                inverse_std(q, var_eps)
+
+        def tensor_mean(q):
+            if q == group[q].start:
+                sums[q] = psum_sum.tile([P, len(group[q]) * PAIR, P], F32, name="sums", tag="sum")
+            else:
+                sums[q] = sums[q - 1]
+            for i in range(PAIR):
+                for n in range(FEATURES // P):
+                    nc.tensor.matmul(
+                        out=sums[q][:, column(q, i).start, :], lhsT=ident_mean[:],
+                        rhs=x_pairs[q][:, i, n * P : (n + 1) * P],
+                        start=(n == 0), stop=(n == FEATURES // P - 1),
+                    )
+
+        def finish_mean(q):
+            if q == group[q].stop - 1:
+                nc.vector.tensor_reduce(out=mean[q][:], in_=sums[q][:], axis=AXIS.X, op=ALU.add)
 
         def normalise(q):
             normed[q] = stage.tile([P, PAIR, FEATURES], BF16, name="normed")
             for i in range(PAIR):
                 nc.vector.tensor_scalar(
                     out=normed[q][:, i, :], in0=x_pairs[q][:, i, :],
-                    scalar1=mean[q][:, i : i + 1], scalar2=rstd[q][:, i : i + 1],
+                    scalar1=mean[q][:, column(q, i)], scalar2=rstd[q][:, column(q, i)],
                     op0=ALU.subtract, op1=ALU.mult,
                 )
 
@@ -362,48 +432,72 @@ def tile_gatingmixeddecoder_pa_t_kernel(tc, z, c, gate_logits, w0, b0, out):
             mixed_exp[q] = flow.tile([P, PAIR, HIDDEN], F32, name="mixed_exp")
             nc.scalar.activation(out=mixed_exp[q][:], in_=mixed[q][:], func=ACT.Exp)
 
-        def elu_and_store(q):
-            below = flow.tile([P, PAIR, HIDDEN], F32)
+        def below_zero(q):
+            below[q] = flow.tile([P, PAIR, HIDDEN], F32, name="below")
             nc.vector.tensor_scalar(
-                out=below[:], in0=mixed_exp[q][:], scalar1=1.0, scalar2=-1.0,
+                out=below[q][:], in0=mixed_exp[q][:], scalar1=1.0, scalar2=-1.0,
                 op0=ALU.min, op1=ALU.add,
             )
+
+        def elu_and_store(q):
             result = flow.tile([P, PAIR, HIDDEN], F32)
-            nc.vector.tensor_tensor(out=result[:], in0=mixed[q][:], in1=below[:], op=ALU.max)
+            nc.vector.tensor_tensor(out=result[:], in0=mixed[q][:], in1=below[q][:], op=ALU.max)
             nc.sync.dma_start(out=out_rows[:, q * PAIR : (q + 1) * PAIR, :], in_=result[:])
 
-        def run(stage_of_pair, q, last=PAIRS):
-            if 0 <= q < last:
+        def run(stage_of_pair, q, first=0, last=PAIRS):
+            if first <= q < last:
                 stage_of_pair(q)
 
-        def scalar_stats(n):
-            if HEAD_TILES + n + 1 < TILES:
-                scalar_mean(HEAD_TILES + n + 1)
-            if HEAD_TILES + n < TILES:
-                scalar_spread(HEAD_TILES + n)
+        def two_pass_tiles(first, last):
+            passes = []
+            for t in range(first, last + 1):
+                if t < last:
+                    passes.append((scalar_mean, t))
+                if t > first:
+                    passes.append((scalar_spread, t - 1))
+            return passes
 
-        scalar_mean(HEAD_TILES)
-        for s in range(-4, PAIRS + 1):
+        passes = two_pass_tiles(HEAD_PAIRS * PAIR, SUMMED_FIRST * PAIR)
+        for t in range(SUMMED_FIRST * PAIR, SUMMED_LAST * PAIR):
+            passes.append((scalar_spread, t))
+        passes.extend(two_pass_tiles(SUMMED_LAST * PAIR, TILES))
+
+        def scalar_stats(count):
+            for taken in range(min(count, len(passes))):
+                stage_of_tile, t = passes[0]
+                passes.remove(passes[0])
+                stage_of_tile(t)
+
+        for s in range(-4, PAIRS + 2):
             run(exponential, s - 1)
             if s == -2:
-                finish_coefficients()
+                for step in coefficient_steps:
+                    step()
                 start_bias_operands()
             run(normalise, s + 2)
             run(transpose, s + 2)
             if s == -2:
                 regroup_weights()
-                finish_bias_operands()
             if s == -1:
                 quantise_weights()
             run(quantise, s + 1)
-            run(bias_product, s + 1)
+            if s == -2:
+                finish_bias_operands()
+            run(below_zero, s - 2)
             run(mix, s)
             run(multiply, s + 1)
-            run(elu_and_store, s - 1)
-            run(vector_stats, s + 4, HEAD_PAIRS)
-            run(regroup, s + 2)
+            run(finish_mean, s + 7, SUMMED_FIRST, SUMMED_LAST)
+            if s == -2:
+                tensor_mean(SUMMED_FIRST)
+            run(tensor_mean, s + 8, SUMMED_FIRST + 1, SUMMED_LAST)
+            run(elu_and_store, s - 2)
             if s + 4 < HEAD_PAIRS:
-                scalar_stats(PAIR * (s + 4))
-                scalar_stats(PAIR * (s + 4) + 1)
+                vector_stats(s + 4, coefficient_steps if s < -2 else [])
+            run(regroup, s + 2)
+            if s == -4:
+                scalar_stats(4)
+            elif 5 <= s < 8:
+                scalar_stats(3)
             else:
-                scalar_stats(HEAD_PAIRS + s + 4)
+                scalar_stats(2)
+            run(bias_product, s + 2)

@@ -30,11 +30,12 @@ WORDS = FEATURES // PACK
 N_COLS = 512
 HALVES = EXPERTS * HIDDEN // N_COLS
 BN_CHUNK = 512
-HEAD_PAIRS = 3
+HEAD_PAIRS = 4
 GROUP = 2
 SUMMED_FIRST = HEAD_PAIRS + GROUP
 SUMMED_PAIRS = 4 * GROUP
 SUMMED_LAST = SUMMED_FIRST + SUMMED_PAIRS
+SUM_COLS = 64
 PIECES = 3
 SLOT = 16
 SLOT_TILES = P // SLOT
@@ -75,11 +76,18 @@ def tile_gatingmixeddecoder_pa_t_kernel(tc, z, c, gate_logits, w0, b0, out):
             nc.sync.dma_start(out=x_pairs[q][:, :, 0:LATENT], in_=z_rows[:, tiles, :])
             nc.sync.dma_start(out=x_pairs[q][:, :, LATENT:FEATURES], in_=c_rows[:, tiles, :])
 
+        def load_tile(t):
+            q, i = t // PAIR, t % PAIR
+            nc.sync.dma_start(out=x_pairs[q][:, i, 0:LATENT], in_=z_rows[:, t, :])
+            nc.sync.dma_start(out=x_pairs[q][:, i, LATENT:FEATURES], in_=c_rows[:, t, :])
+
         w_raw = keep.tile([P, EXPERTS, PASSES * 2, 2 * HIDDEN], BF16)
 
-        for q in range(2):
-            load_pair(q)
-            load_pair(HEAD_PAIRS + q)
+        for t in range(PAIR):
+            load_tile(t)
+        load_pair(HEAD_PAIRS)
+        load_pair(1)
+        load_pair(HEAD_PAIRS + 1)
         for x in range(EXPERTS):
             nc.sync.dma_start(
                 out=w_raw[:, x, :, :],
@@ -88,7 +96,9 @@ def tile_gatingmixeddecoder_pa_t_kernel(tc, z, c, gate_logits, w0, b0, out):
         for q in range(2, HEAD_PAIRS):
             load_pair(q)
             load_pair(HEAD_PAIRS + q)
-        for q in range(2 * HEAD_PAIRS, PAIRS):
+        for q in range(SUMMED_LAST, PAIRS):
+            load_pair(q)
+        for q in range(2 * HEAD_PAIRS, SUMMED_LAST):
             load_pair(q)
 
         ident_f32 = keep.tile([P, P], F32)
@@ -230,6 +240,7 @@ def tile_gatingmixeddecoder_pa_t_kernel(tc, z, c, gate_logits, w0, b0, out):
         grouped = {}
         codes = {}
         products = {}
+        bias_sums = {}
         bias_mix = {}
         mixed = {}
         mixed_exp = {}
@@ -330,15 +341,17 @@ def tile_gatingmixeddecoder_pa_t_kernel(tc, z, c, gate_logits, w0, b0, out):
 
         def tensor_mean(q):
             if q == group[q].start:
-                sums[q] = psum_sum.tile([P, len(group[q]) * PAIR, P], F32, name="sums", tag="sum")
+                sums[q] = psum_sum.tile(
+                    [P, len(group[q]) * PAIR, SUM_COLS], F32, name="sums", tag="sum"
+                )
             else:
                 sums[q] = sums[q - 1]
             for i in range(PAIR):
-                for n in range(FEATURES // P):
+                for n in range(FEATURES // SUM_COLS):
                     nc.tensor.matmul(
                         out=sums[q][:, column(q, i).start, :], lhsT=ident_mean[:],
-                        rhs=x_pairs[q][:, i, n * P : (n + 1) * P],
-                        start=(n == 0), stop=(n == FEATURES // P - 1),
+                        rhs=x_pairs[q][:, i, n * SUM_COLS : (n + 1) * SUM_COLS],
+                        start=(n == 0), stop=(n == FEATURES // SUM_COLS - 1),
                     )
 
         def finish_mean(q):
@@ -387,15 +400,17 @@ def tile_gatingmixeddecoder_pa_t_kernel(tc, z, c, gate_logits, w0, b0, out):
             codes[q] = (words, plane)
 
         def bias_product(q):
-            both = psum_bias.tile([P, PAIR, HIDDEN], F32, tag="bias")
+            bias_sums[q] = psum_bias.tile([P, PAIR, HIDDEN], F32, name="bias_sums", tag="bias")
             for i in range(PAIR):
                 t = q * PAIR + i
                 nc.tensor.matmul(
-                    out=both[:, i, :], lhsT=pieces_t[:, t // SLOT_TILES, :],
+                    out=bias_sums[q][:, i, :], lhsT=pieces_t[:, t // SLOT_TILES, :],
                     rhs=bias_slot[:, t % SLOT_TILES, :], start=True, stop=True,
                 )
+
+        def copy_bias(q):
             bias_mix[q] = flow.tile([P, PAIR, HIDDEN], F32, name="bias_mix")
-            nc.scalar.copy(out=bias_mix[q][:], in_=both[:])
+            nc.scalar.copy(out=bias_mix[q][:], in_=bias_sums[q][:])
 
         def multiply(q):
             words, plane = codes[q]
@@ -432,6 +447,18 @@ def tile_gatingmixeddecoder_pa_t_kernel(tc, z, c, gate_logits, w0, b0, out):
             mixed_exp[q] = flow.tile([P, PAIR, HIDDEN], F32, name="mixed_exp")
             nc.scalar.activation(out=mixed_exp[q][:], in_=mixed[q][:], func=ACT.Exp)
 
+        def relu(q):
+            below[q] = flow.tile([P, PAIR, HIDDEN], F32, name="below")
+            nc.scalar.activation(out=below[q][:], in_=mixed[q][:], func=ACT.Relu)
+
+        def relu_and_store(q):
+            result = flow.tile([P, PAIR, HIDDEN], F32)
+            nc.vector.scalar_tensor_tensor(
+                out=result[:], in0=mixed_exp[q][:], scalar=1.0, in1=below[q][:],
+                op0=ALU.subtract, op1=ALU.min,
+            )
+            nc.sync.dma_start(out=out_rows[:, q * PAIR : (q + 1) * PAIR, :], in_=result[:])
+
         def below_zero(q):
             below[q] = flow.tile([P, PAIR, HIDDEN], F32, name="below")
             nc.vector.tensor_scalar(
@@ -458,9 +485,10 @@ def tile_gatingmixeddecoder_pa_t_kernel(tc, z, c, gate_logits, w0, b0, out):
             return passes
 
         passes = two_pass_tiles(HEAD_PAIRS * PAIR, SUMMED_FIRST * PAIR)
-        for t in range(SUMMED_FIRST * PAIR, SUMMED_LAST * PAIR):
+        for t in range(SUMMED_LAST * PAIR, TILES):
+            passes.append((scalar_mean, t))
+        for t in range(SUMMED_FIRST * PAIR, TILES):
             passes.append((scalar_spread, t))
-        passes.extend(two_pass_tiles(SUMMED_LAST * PAIR, TILES))
 
         def scalar_stats(count):
             for taken in range(min(count, len(passes))):
@@ -470,6 +498,7 @@ def tile_gatingmixeddecoder_pa_t_kernel(tc, z, c, gate_logits, w0, b0, out):
 
         for s in range(-4, PAIRS + 2):
             run(exponential, s - 1)
+            run(relu, s - 1, 11)
             if s == -2:
                 for step in coefficient_steps:
                     step()
@@ -483,21 +512,21 @@ def tile_gatingmixeddecoder_pa_t_kernel(tc, z, c, gate_logits, w0, b0, out):
             run(quantise, s + 1)
             if s == -2:
                 finish_bias_operands()
-            run(below_zero, s - 2)
+            run(bias_product, s + 2)
+            run(below_zero, s - 2, last=11)
             run(mix, s)
             run(multiply, s + 1)
             run(finish_mean, s + 7, SUMMED_FIRST, SUMMED_LAST)
-            if s == -2:
-                tensor_mean(SUMMED_FIRST)
-            run(tensor_mean, s + 8, SUMMED_FIRST + 1, SUMMED_LAST)
-            run(elu_and_store, s - 2)
+            run(tensor_mean, s + 8, SUMMED_FIRST, SUMMED_LAST)
+            run(elu_and_store, s - 2, last=11)
+            run(relu_and_store, s - 2, 11)
             if s + 4 < HEAD_PAIRS:
                 vector_stats(s + 4, coefficient_steps if s < -2 else [])
             run(regroup, s + 2)
             if s == -4:
                 scalar_stats(4)
-            elif 5 <= s < 8:
+            elif s == -1:
                 scalar_stats(3)
             else:
                 scalar_stats(2)
-            run(bias_product, s + 2)
+            run(copy_bias, s + 2)

@@ -115,6 +115,24 @@ def tile_gatingmixeddecoder_pa_t_kernel(tc, z, c, gate_logits, w0, b0, out):
         eps = keep.tile([P, 1], F32)
         nc.vector.memset(eps[:], EPS)
 
+        spread = keep.tile([P, P // EXPERTS, EXPERTS], BF16)
+        nc.vector.tensor_copy(
+            out=spread[:],
+            in_=ident_bf16[:, 0:EXPERTS].unsqueeze(1).to_broadcast([P, P // EXPERTS, EXPERTS]),
+        )
+        bias_ps = psum_bias.tile([P, HIDDEN], F32, tag="bias")
+        nc.tensor.matmul(
+            out=bias_ps[:], lhsT=spread[:].rearrange("p a e -> p (a e)"), rhs=bias_rows[:],
+            start=True, stop=True,
+        )
+        in_slot = keep.tile([P, SLOT_TILES], F32)
+        nc.vector.tensor_reduce(
+            out=in_slot[:], in_=ident_f32[:].rearrange("p (b j) -> p b j", j=SLOT),
+            axis=AXIS.X, op=ALU.add,
+        )
+        pieces = keep.tile([P, TILES, SLOT], BF16)
+        nc.vector.memset(pieces[:], 0.0)
+
         wide = [P, TILES, EXPERTS]
         gate_max = keep.tile([P, TILES], F32)
         nc.vector.tensor_reduce(out=gate_max[:], in_=gate[:], axis=AXIS.X, op=ALU.max)
@@ -125,15 +143,18 @@ def tile_gatingmixeddecoder_pa_t_kernel(tc, z, c, gate_logits, w0, b0, out):
         )
         nc.scalar.activation(out=gate_exp[:], in_=gate_exp[:], func=ACT.Exp)
         coeff = keep.tile(wide, F32)
-        pieces = keep.tile([P, TILES, SLOT], BF16)
         blocks = TILES // SLOT_TILES
         pieces_ps = psum_sum.tile([P, blocks, P], BF16, tag="sum")
         pieces_t = keep.tile([P, blocks, P], BF16)
-        spread = keep.tile([P, P // EXPERTS, EXPERTS], BF16)
-        bias_ps = psum_bias.tile([P, HIDDEN], F32, tag="bias")
+
         bias_all = keep.tile([P, HIDDEN], BF16)
-        in_slot = keep.tile([P, SLOT_TILES], F32)
+        nc.scalar.copy(out=bias_all[:], in_=bias_ps[:])
         bias_slot = keep.tile([P, SLOT_TILES, HIDDEN], BF16)
+        for b in range(SLOT_TILES):
+            nc.gpsimd.tensor_scalar(
+                out=bias_slot[:, b, :], in0=bias_all[:], scalar1=in_slot[:, b : b + 1],
+                scalar2=0.0, op0=ALU.mult, op1=ALU.add,
+            )
 
         gate_sum = keep.tile([P, TILES], F32)
         gate_inv = keep.tile([P, TILES], F32)
@@ -153,7 +174,6 @@ def tile_gatingmixeddecoder_pa_t_kernel(tc, z, c, gate_logits, w0, b0, out):
                 out=coeff[:], in0=gate_exp[:], in1=gate_inv[:].unsqueeze(2).to_broadcast(wide),
                 op=ALU.mult,
             ),
-            lambda: nc.vector.memset(pieces[:], 0.0),
         ]
         for i in range(PIECES):
             coefficient_steps.append(
@@ -166,7 +186,7 @@ def tile_gatingmixeddecoder_pa_t_kernel(tc, z, c, gate_logits, w0, b0, out):
                     )
                 )
 
-        def start_bias_operands():
+        def transpose_pieces():
             for a in range(blocks):
                 nc.tensor.transpose(
                     pieces_ps[:, a, :],
@@ -175,29 +195,9 @@ def tile_gatingmixeddecoder_pa_t_kernel(tc, z, c, gate_logits, w0, b0, out):
                     ),
                     ident_bf16[:],
                 )
-            nc.vector.tensor_copy(
-                out=spread[:],
-                in_=ident_bf16[:, 0:EXPERTS].unsqueeze(1).to_broadcast(
-                    [P, P // EXPERTS, EXPERTS]
-                ),
-            )
-            nc.tensor.matmul(
-                out=bias_ps[:], lhsT=spread[:].rearrange("p a e -> p (a e)"), rhs=bias_rows[:],
-                start=True, stop=True,
-            )
-            nc.vector.tensor_reduce(
-                out=in_slot[:], in_=ident_f32[:].rearrange("p (b j) -> p b j", j=SLOT),
-                axis=AXIS.X, op=ALU.add,
-            )
 
-        def finish_bias_operands():
+        def copy_pieces():
             nc.vector.tensor_copy(out=pieces_t[:], in_=pieces_ps[:])
-            nc.vector.tensor_copy(out=bias_all[:], in_=bias_ps[:])
-            for b in range(SLOT_TILES):
-                nc.vector.tensor_scalar(
-                    out=bias_slot[:, b, :], in0=bias_all[:], scalar1=in_slot[:, b : b + 1],
-                    scalar2=None, op0=ALU.mult,
-                )
 
         w_codes = keep.tile([P, PASSES, EXPERTS * HIDDEN], U32, align_bytes=64)
         w_scales = keep.tile([P, PASSES, EXPERTS * HIDDEN], U8, align_bytes=64)
@@ -498,11 +498,11 @@ def tile_gatingmixeddecoder_pa_t_kernel(tc, z, c, gate_logits, w0, b0, out):
 
         for s in range(-4, PAIRS + 2):
             run(exponential, s - 1)
-            run(relu, s - 1, 11)
+            run(relu, s - 1, 10)
             if s == -2:
                 for step in coefficient_steps:
                     step()
-                start_bias_operands()
+                transpose_pieces()
             run(normalise, s + 2)
             run(transpose, s + 2)
             if s == -2:
@@ -511,22 +511,19 @@ def tile_gatingmixeddecoder_pa_t_kernel(tc, z, c, gate_logits, w0, b0, out):
                 quantise_weights()
             run(quantise, s + 1)
             if s == -2:
-                finish_bias_operands()
+                copy_pieces()
             run(bias_product, s + 2)
-            run(below_zero, s - 2, last=11)
+            run(below_zero, s - 2, last=10)
             run(mix, s)
             run(multiply, s + 1)
             run(finish_mean, s + 7, SUMMED_FIRST, SUMMED_LAST)
             run(tensor_mean, s + 8, SUMMED_FIRST, SUMMED_LAST)
-            run(elu_and_store, s - 2, last=11)
-            run(relu_and_store, s - 2, 11)
+            run(elu_and_store, s - 2, last=10)
+            run(relu_and_store, s - 2, 10)
             if s + 4 < HEAD_PAIRS:
                 vector_stats(s + 4, coefficient_steps if s < -2 else [])
+            if s > -4:
+                scalar_stats(1)
             run(regroup, s + 2)
-            if s == -4:
-                scalar_stats(4)
-            elif s == -1:
-                scalar_stats(3)
-            else:
-                scalar_stats(2)
+            scalar_stats(4 if s == -4 else 2 if s == -1 else 1)
             run(copy_bias, s + 2)

@@ -52,7 +52,7 @@ def tile_gatingmixeddecoder_pa_t_kernel(tc, z, c, gate_logits, w0, b0, out):
     with ExitStack() as ctx:
         keep = ctx.enter_context(tc.tile_pool(name="keep", bufs=1))
         stage = ctx.enter_context(tc.tile_pool(name="stage", bufs=2))
-        flow = ctx.enter_context(tc.tile_pool(name="flow", bufs=4))
+        flow = ctx.enter_context(tc.tile_pool(name="flow", bufs=3))
         small = ctx.enter_context(tc.tile_pool(name="small", bufs=12))
         psum_sum = ctx.enter_context(tc.psum_pool(name="psum_sum", bufs=1))
         psum_xt = ctx.enter_context(tc.psum_pool(name="psum_xt", bufs=2))
@@ -112,6 +112,8 @@ def tile_gatingmixeddecoder_pa_t_kernel(tc, z, c, gate_logits, w0, b0, out):
         )
         neg_half = keep.tile([P, GROUP * PAIR], F32)
         nc.vector.memset(neg_half[:], -0.5)
+        one = keep.tile([P, 1], F32)
+        nc.vector.memset(one[:], 1.0)
         eps = keep.tile([P, 1], F32)
         nc.vector.memset(eps[:], EPS)
 
@@ -253,6 +255,7 @@ def tile_gatingmixeddecoder_pa_t_kernel(tc, z, c, gate_logits, w0, b0, out):
         mean = {}
         rstd = {}
         sums = {}
+        complete = []
         spreads = {}
         chunks = {}
         for first, last in ((0, HEAD_PAIRS), (HEAD_PAIRS, PAIRS)):
@@ -332,12 +335,17 @@ def tile_gatingmixeddecoder_pa_t_kernel(tc, z, c, gate_logits, w0, b0, out):
                 scale=-1.0, accum_out=spreads[q][:, column(q, i)],
             )
             if t == group[q].stop * PAIR - 1:
+                complete.append(q)
+
+        def finish_spreads():
+            for q in complete:
                 var_eps = small.tile([P, len(group[q]) * PAIR], F32)
                 nc.scalar.activation(
                     out=var_eps[:], in_=spreads[q][:], func=ACT.Identity, bias=eps[:],
                     scale=1.0 / FEATURES,
                 )
                 inverse_std(q, var_eps)
+            complete.clear()
 
         def tensor_mean(q):
             if q == group[q].start:
@@ -347,12 +355,25 @@ def tile_gatingmixeddecoder_pa_t_kernel(tc, z, c, gate_logits, w0, b0, out):
             else:
                 sums[q] = sums[q - 1]
             for i in range(PAIR):
-                for n in range(FEATURES // SUM_COLS):
-                    nc.tensor.matmul(
-                        out=sums[q][:, column(q, i).start, :], lhsT=ident_mean[:],
-                        rhs=x_pairs[q][:, i, n * SUM_COLS : (n + 1) * SUM_COLS],
-                        start=(n == 0), stop=(n == FEATURES // SUM_COLS - 1),
-                    )
+                sum_features(sums[q][:, column(q, i).start, :], q * PAIR + i)
+
+        def sum_features(target, t):
+            for n in range(FEATURES // SUM_COLS):
+                nc.tensor.matmul(
+                    out=target, lhsT=ident_mean[:],
+                    rhs=x_tile(t)[:, n * SUM_COLS : (n + 1) * SUM_COLS],
+                    start=(n == 0), stop=(n == FEATURES // SUM_COLS - 1),
+                )
+
+        def tensor_mean_single(t):
+            sums[t] = psum_sum.tile([P, SUM_COLS], F32, name="sums1", tag="sum")
+            sum_features(sums[t][:], t)
+
+        def finish_mean_single(t):
+            q, i = t // PAIR, t % PAIR
+            nc.vector.tensor_reduce(
+                out=mean[q][:, column(q, i)], in_=sums[t][:], axis=AXIS.X, op=ALU.add
+            )
 
         def finish_mean(q):
             if q == group[q].stop - 1:
@@ -459,6 +480,32 @@ def tile_gatingmixeddecoder_pa_t_kernel(tc, z, c, gate_logits, w0, b0, out):
             )
             nc.sync.dma_start(out=out_rows[:, q * PAIR : (q + 1) * PAIR, :], in_=result[:])
 
+        def elu_beside_vector(q):
+            lack = flow.tile([P, PAIR, HIDDEN], F32)
+            nc.scalar.activation(
+                out=lack[:], in_=mixed_exp[q][:], func=ACT.Relu, bias=one[:], scale=-1.0
+            )
+            result = flow.tile([P, PAIR, HIDDEN], F32, name="result_beside")
+            nc.gpsimd.tensor_tensor(
+                out=result[:], in0=below[q][:], in1=lack[:], op=ALU.subtract
+            )
+            nc.sync.dma_start(out=out_rows[:, q * PAIR : (q + 1) * PAIR, :], in_=result[:])
+
+        def last_elu_and_store(q):
+            ramp = flow.tile([P, PAIR, HIDDEN], F32)
+            nc.vector.tensor_scalar(
+                out=ramp[:], in0=mixed[q][:], scalar1=0.0, scalar2=None, op0=ALU.max
+            )
+            for i in range(PAIR):
+                power = flow.tile([P, HIDDEN], F32, name="power%d" % i)
+                nc.scalar.activation(out=power[:], in_=mixed[q][:, i, :], func=ACT.Exp)
+                result = flow.tile([P, HIDDEN], F32, name="result%d" % i)
+                nc.vector.scalar_tensor_tensor(
+                    out=result[:], in0=power[:], scalar=1.0, in1=ramp[:, i, :],
+                    op0=ALU.subtract, op1=ALU.min,
+                )
+                nc.sync.dma_start(out=out_rows[:, q * PAIR + i, :], in_=result[:])
+
         def below_zero(q):
             below[q] = flow.tile([P, PAIR, HIDDEN], F32, name="below")
             nc.vector.tensor_scalar(
@@ -485,7 +532,7 @@ def tile_gatingmixeddecoder_pa_t_kernel(tc, z, c, gate_logits, w0, b0, out):
             return passes
 
         passes = two_pass_tiles(HEAD_PAIRS * PAIR, SUMMED_FIRST * PAIR)
-        for t in range(SUMMED_LAST * PAIR, TILES):
+        for t in range(SUMMED_LAST * PAIR + 1, TILES):
             passes.append((scalar_mean, t))
         for t in range(SUMMED_FIRST * PAIR, TILES):
             passes.append((scalar_spread, t))
@@ -496,9 +543,10 @@ def tile_gatingmixeddecoder_pa_t_kernel(tc, z, c, gate_logits, w0, b0, out):
                 passes.remove(passes[0])
                 stage_of_tile(t)
 
-        for s in range(-4, PAIRS + 2):
-            run(exponential, s - 1)
-            run(relu, s - 1, 10)
+        for s in range(-4, PAIRS + 1):
+            run(exponential, s - 1, last=PAIRS - 1)
+            run(relu, s - 1, 9, PAIRS - 1)
+            run(elu_beside_vector, s - 1, 13, PAIRS - 1)
             if s == -2:
                 for step in coefficient_steps:
                     step()
@@ -513,17 +561,26 @@ def tile_gatingmixeddecoder_pa_t_kernel(tc, z, c, gate_logits, w0, b0, out):
             if s == -2:
                 copy_pieces()
             run(bias_product, s + 2)
-            run(below_zero, s - 2, last=10)
+            run(below_zero, s - 2, last=9)
             run(mix, s)
             run(multiply, s + 1)
-            run(finish_mean, s + 7, SUMMED_FIRST, SUMMED_LAST)
-            run(tensor_mean, s + 8, SUMMED_FIRST, SUMMED_LAST)
-            run(elu_and_store, s - 2, last=10)
-            run(relu_and_store, s - 2, 10)
+            run(finish_mean, s + 8, SUMMED_FIRST, SUMMED_LAST)
+            if s == -2:
+                tensor_mean(SUMMED_FIRST)
+            run(tensor_mean, s + 9, SUMMED_FIRST + 1, SUMMED_LAST)
+            if s == 5:
+                tensor_mean_single(SUMMED_LAST * PAIR)
+            if s == 6:
+                finish_mean_single(SUMMED_LAST * PAIR)
+            run(elu_and_store, s - 2, last=9)
+            run(relu_and_store, s - 2, 9, 13)
             if s + 4 < HEAD_PAIRS:
                 vector_stats(s + 4, coefficient_steps if s < -2 else [])
             if s > -4:
                 scalar_stats(1)
             run(regroup, s + 2)
+            finish_spreads()
             scalar_stats(4 if s == -4 else 2 if s == -1 else 1)
             run(copy_bias, s + 2)
+            finish_spreads()
+            run(last_elu_and_store, s - 1, PAIRS - 1)

@@ -36,6 +36,8 @@ SUMMED_FIRST = HEAD_PAIRS + GROUP
 SUMMED_PAIRS = 4 * GROUP
 SUMMED_LAST = SUMMED_FIRST + SUMMED_PAIRS
 SUM_COLS = 64
+BESIDE_FIRST = 4
+BESIDE_LAST = 16
 PIECES = 3
 SLOT = 16
 SLOT_TILES = P // SLOT
@@ -53,6 +55,7 @@ def tile_gatingmixeddecoder_pa_t_kernel(tc, z, c, gate_logits, w0, b0, out):
         keep = ctx.enter_context(tc.tile_pool(name="keep", bufs=1))
         stage = ctx.enter_context(tc.tile_pool(name="stage", bufs=2))
         flow = ctx.enter_context(tc.tile_pool(name="flow", bufs=3))
+        normed_pool = ctx.enter_context(tc.tile_pool(name="normed_pool", bufs=3))
         small = ctx.enter_context(tc.tile_pool(name="small", bufs=12))
         psum_sum = ctx.enter_context(tc.psum_pool(name="psum_sum", bufs=1))
         psum_xt = ctx.enter_context(tc.psum_pool(name="psum_xt", bufs=2))
@@ -379,9 +382,26 @@ def tile_gatingmixeddecoder_pa_t_kernel(tc, z, c, gate_logits, w0, b0, out):
             if q == group[q].stop - 1:
                 nc.vector.tensor_reduce(out=mean[q][:], in_=sums[q][:], axis=AXIS.X, op=ALU.add)
 
+        def normalise_beside_mix(q):
+            i = PAIR - 1
+            normed[q] = normed_pool.tile([P, PAIR, FEATURES], BF16, name="normed")
+            offset = small.tile([P, 1], F32)
+            nc.vector.scalar_tensor_tensor(
+                out=offset[:], in0=mean[q][:, column(q, i)], scalar=-1.0,
+                in1=rstd[q][:, column(q, i)], op0=ALU.mult, op1=ALU.mult,
+            )
+            nc.gpsimd.tensor_scalar(
+                out=normed[q][:, i, :], in0=x_pairs[q][:, i, :],
+                scalar1=rstd[q][:, column(q, i)], scalar2=offset[:], op0=ALU.mult, op1=ALU.add,
+            )
+
         def normalise(q):
-            normed[q] = stage.tile([P, PAIR, FEATURES], BF16, name="normed")
-            for i in range(PAIR):
+            if BESIDE_FIRST <= q < BESIDE_LAST:
+                beside = 1
+            else:
+                beside = 0
+                normed[q] = normed_pool.tile([P, PAIR, FEATURES], BF16, name="normed")
+            for i in range(PAIR - beside):
                 nc.vector.tensor_scalar(
                     out=normed[q][:, i, :], in0=x_pairs[q][:, i, :],
                     scalar1=mean[q][:, column(q, i)], scalar2=rstd[q][:, column(q, i)],
@@ -562,6 +582,7 @@ def tile_gatingmixeddecoder_pa_t_kernel(tc, z, c, gate_logits, w0, b0, out):
                 copy_pieces()
             run(bias_product, s + 2)
             run(below_zero, s - 2, last=9)
+            run(normalise_beside_mix, s + 3, BESIDE_FIRST, BESIDE_LAST)
             run(mix, s)
             run(multiply, s + 1)
             run(finish_mean, s + 8, SUMMED_FIRST, SUMMED_LAST)

from contextlib import ExitStack

import concourse.mybir as mybir
from concourse.masks import make_identity

F32 = mybir.dt.float32
BF16 = mybir.dt.bfloat16
U32 = mybir.dt.uint32
U8 = mybir.dt.uint8
FP8X4 = mybir.dt.float8_e4m3fn_x4
ALU = mybir.AluOpType
ACT = mybir.ActivationFunctionType
AXIS = mybir.AxisListType

P = 128
ROWS = 4096
LATENT = 256
FEATURES = 1024
EXPERTS = 4
HIDDEN = 256
EPS = 1e-5

TILES = ROWS // P
PAIR = 2
PAIRS = TILES // PAIR
PACK = 4
K_PASS = P * PACK
PASSES = FEATURES // K_PASS
WORDS = FEATURES // PACK
N_COLS = 512
HALVES = EXPERTS * HIDDEN // N_COLS
BN_CHUNK = 512
HEAD_PAIRS = 4
GROUP = 2
SUMMED_FIRST = HEAD_PAIRS + GROUP
SUMMED_PAIRS = 4 * GROUP
SUMMED_LAST = SUMMED_FIRST + SUMMED_PAIRS
SUM_COLS = 64
BESIDE_FIRST = 4
BESIDE_LAST = 16
PIECES = 3
SLOT = 16
SLOT_TILES = P // SLOT

FLOPS = 2 * ROWS * FEATURES * EXPERTS * HIDDEN


def tile_gatingmixeddecoder_pa_t_kernel(tc, z, c, gate_logits, w0, b0, out):
    nc = tc.nc
    z_rows = z.rearrange("(p t) k -> p t k", t=TILES)
    c_rows = c.rearrange("(p t) k -> p t k", t=TILES)
    out_rows = out.rearrange("(p t) h -> p t h", t=TILES)

    with ExitStack() as ctx:
        keep = ctx.enter_context(tc.tile_pool(name="keep", bufs=1))
        stage = ctx.enter_context(tc.tile_pool(name="stage", bufs=2))
        flow = ctx.enter_context(tc.tile_pool(name="flow", bufs=3))
        normed_pool = ctx.enter_context(tc.tile_pool(name="normed_pool", bufs=3))
        small = ctx.enter_context(tc.tile_pool(name="small", bufs=12))
        psum_sum = ctx.enter_context(tc.psum_pool(name="psum_sum", bufs=1))
        psum_xt = ctx.enter_context(tc.psum_pool(name="psum_xt", bufs=2))
        psum_y = ctx.enter_context(tc.psum_pool(name="psum_y", bufs=2))
        psum_bias = ctx.enter_context(tc.psum_pool(name="psum_bias", bufs=1))
        ctx.enter_context(tc.manual_schedule())

        gate = keep.tile([P, TILES, EXPERTS], BF16)
        nc.scalar.dma_start(out=gate[:], in_=gate_logits.rearrange("(p t) e -> p t e", t=TILES))

        bias_rows = keep.tile([P, HIDDEN], BF16)
        nc.vector.memset(bias_rows[:], 0.0)
        nc.scalar.dma_start(out=bias_rows[0:EXPERTS, :], in_=b0)

        x_pairs = [
            keep.tile([P, PAIR, FEATURES], BF16, name="x_pair%d" % q) for q in range(PAIRS)
        ]

        def load_pair(q):
            tiles = slice(q * PAIR, (q + 1) * PAIR)
            nc.sync.dma_start(out=x_pairs[q][:, :, 0:LATENT], in_=z_rows[:, tiles, :])
            nc.sync.dma_start(out=x_pairs[q][:, :, LATENT:FEATURES], in_=c_rows[:, tiles, :])

        def load_tile(t):
            q, i = t // PAIR, t % PAIR
            nc.sync.dma_start(out=x_pairs[q][:, i, 0:LATENT], in_=z_rows[:, t, :])
            nc.sync.dma_start(out=x_pairs[q][:, i, LATENT:FEATURES], in_=c_rows[:, t, :])

        w_raw = keep.tile([P, EXPERTS, PASSES * 2, 2 * HIDDEN], BF16)

        for t in range(PAIR):
            load_tile(t)
        load_pair(HEAD_PAIRS)
        load_pair(1)
        load_pair(HEAD_PAIRS + 1)
        for x in range(EXPERTS):
            nc.sync.dma_start(
                out=w_raw[:, x, :, :],
                in_=w0[x].rearrange("(gu p e) h -> p gu (e h)", p=P, e=2),
            )
        for q in range(2, HEAD_PAIRS):
            load_pair(q)
            load_pair(HEAD_PAIRS + q)
        for q in range(SUMMED_LAST, PAIRS):
            load_pair(q)
        for q in range(2 * HEAD_PAIRS, SUMMED_LAST):
            load_pair(q)

        ident_f32 = keep.tile([P, P], F32)
        make_identity(nc, ident_f32[:])
        ident_bf16 = keep.tile([P, P], BF16)
        make_identity(nc, ident_bf16[:])
        ident_mean = keep.tile([P, P], BF16)
        nc.vector.tensor_scalar(
            out=ident_mean[:], in0=ident_bf16[:], scalar1=1.0 / FEATURES, scalar2=None,
            op0=ALU.mult,
        )
        neg_half = keep.tile([P, GROUP * PAIR], F32)
        nc.vector.memset(neg_half[:], -0.5)
        one = keep.tile([P, 1], F32)
        nc.vector.memset(one[:], 1.0)
        eps = keep.tile([P, 1], F32)
        nc.vector.memset(eps[:], EPS)

        spread = keep.tile([P, P // EXPERTS, EXPERTS], BF16)
        nc.vector.tensor_copy(
            out=spread[:],
            in_=ident_bf16[:, 0:EXPERTS].unsqueeze(1).to_broadcast([P, P // EXPERTS, EXPERTS]),
        )
        bias_ps = psum_bias.tile([P, HIDDEN], F32, tag="bias")
        nc.tensor.matmul(
            out=bias_ps[:], lhsT=spread[:].rearrange("p a e -> p (a e)"), rhs=bias_rows[:],
            start=True, stop=True,
        )
        in_slot = keep.tile([P, SLOT_TILES], F32)
        nc.vector.tensor_reduce(
            out=in_slot[:], in_=ident_f32[:].rearrange("p (b j) -> p b j", j=SLOT),
            axis=AXIS.X, op=ALU.add,
        )
        pieces = keep.tile([P, TILES, SLOT], BF16)
        nc.vector.memset(pieces[:], 0.0)

        wide = [P, TILES, EXPERTS]
        gate_max = keep.tile([P, TILES], F32)
        nc.vector.tensor_reduce(out=gate_max[:], in_=gate[:], axis=AXIS.X, op=ALU.max)
        gate_exp = keep.tile(wide, F32)
        nc.vector.tensor_tensor(
            out=gate_exp[:], in0=gate[:], in1=gate_max[:].unsqueeze(2).to_broadcast(wide),
            op=ALU.subtract,
        )
        nc.scalar.activation(out=gate_exp[:], in_=gate_exp[:], func=ACT.Exp)
        coeff = keep.tile(wide, F32)
        blocks = TILES // SLOT_TILES
        pieces_ps = psum_sum.tile([P, blocks, P], BF16, tag="sum")
        pieces_t = keep.tile([P, blocks, P], BF16)

        bias_all = keep.tile([P, HIDDEN], BF16)
        nc.scalar.copy(out=bias_all[:], in_=bias_ps[:])
        bias_slot = keep.tile([P, SLOT_TILES, HIDDEN], BF16)
        for b in range(SLOT_TILES):
            nc.gpsimd.tensor_scalar(
                out=bias_slot[:, b, :], in0=bias_all[:], scalar1=in_slot[:, b : b + 1],
                scalar2=0.0, op0=ALU.mult, op1=ALU.add,
            )

        gate_sum = keep.tile([P, TILES], F32)
        gate_inv = keep.tile([P, TILES], F32)
        rests = [coeff]
        for i in range(PIECES - 1):
            rests.append(keep.tile(wide, F32, name="rest%d" % i))

        def piece(i):
            return pieces[:, :, i * EXPERTS : (i + 1) * EXPERTS]

        coefficient_steps = [
            lambda: nc.vector.tensor_reduce(
                out=gate_sum[:], in_=gate_exp[:], axis=AXIS.X, op=ALU.add
            ),
            lambda: nc.vector.reciprocal(out=gate_inv[:], in_=gate_sum[:]),
            lambda: nc.vector.tensor_tensor(
                out=coeff[:], in0=gate_exp[:], in1=gate_inv[:].unsqueeze(2).to_broadcast(wide),
                op=ALU.mult,
            ),
        ]
        for i in range(PIECES):
            coefficient_steps.append(
                lambda i=i: nc.vector.tensor_copy(out=piece(i), in_=rests[i][:])
            )
            if i < PIECES - 1:
                coefficient_steps.append(
                    lambda i=i: nc.vector.tensor_tensor(
                        out=rests[i + 1][:], in0=rests[i][:], in1=piece(i), op=ALU.subtract
                    )
                )

        def transpose_pieces():
            for a in range(blocks):
                nc.tensor.transpose(
                    pieces_ps[:, a, :],
                    pieces[:, a * SLOT_TILES : (a + 1) * SLOT_TILES, :].rearrange(
                        "p b j -> p (b j)"
                    ),
                    ident_bf16[:],
                )

        def copy_pieces():
            nc.vector.tensor_copy(out=pieces_t[:], in_=pieces_ps[:])

        w_codes = keep.tile([P, PASSES, EXPERTS * HIDDEN], U32, align_bytes=64)
        w_scales = keep.tile([P, PASSES, EXPERTS * HIDDEN], U8, align_bytes=64)

        per_half = EXPERTS // HALVES
        w_grouped = {}

        def regroup_weights():
            for half in range(HALVES):
                for g in range(PASSES):
                    w_grouped[g, half] = keep.tile(
                        [P, per_half, HIDDEN, PACK], BF16, name="w_grouped%d%d" % (g, half),
                        align_bytes=64,
                    )
                    for i in range(per_half):
                        planes = w_raw[:, half * per_half + i, 2 * g : 2 * g + 2, :].rearrange(
                            "p u (e h) -> p (u e) h", e=2
                        )
                        source = planes.rearrange("p j (n i) -> p n j i", i=4)
                        target = w_grouped[g, half][:, i, :, :].rearrange(
                            "p (n i) j -> p n j i", i=4
                        )
                        if i % 2 == 0:
                            nc.vector.tensor_copy(out=target, in_=source)
                        else:
                            nc.scalar.copy(out=target, in_=source)

        def quantise_weights():
            for half in range(HALVES):
                for g in range(PASSES):
                    cols = slice(half * N_COLS, (half + 1) * N_COLS)
                    nc.vector.quantize_mx(
                        out=w_codes[:, g, cols].bitcast(FP8X4),
                        scales=w_scales[:, g, cols],
                        in_=w_grouped[g, half][:].rearrange("p x h j -> p (x h j)"),
                    )

        normed = {}
        turned = {}
        grouped = {}
        codes = {}
        products = {}
        bias_sums = {}
        bias_mix = {}
        mixed = {}
        mixed_exp = {}
        below = {}

        def x_tile(t):
            return x_pairs[t // PAIR][:, t % PAIR, :]

        group = {}
        mean = {}
        rstd = {}
        sums = {}
        complete = []
        spreads = {}
        chunks = {}
        for first, last in ((0, HEAD_PAIRS), (HEAD_PAIRS, PAIRS)):
            for start in range(first, last, GROUP):
                members = range(start, min(start + GROUP, last))
                columns = len(members) * PAIR
                group_mean = keep.tile([P, columns], F32, name="mean%d" % start)
                group_rstd = keep.tile([P, columns], F32, name="rstd%d" % start)
                for q in members:
                    group[q], mean[q], rstd[q] = members, group_mean, group_rstd

        def column(q, i):
            return slice((q - group[q].start) * PAIR + i, (q - group[q].start) * PAIR + i + 1)

        def inverse_std(q, var_eps):
            nc.gpsimd.tensor_tensor(
                out=rstd[q][:], in0=var_eps[:], in1=neg_half[:, 0 : len(group[q]) * PAIR],
                op=ALU.pow,
            )

        def vector_stats(q, between):
            per_tile = FEATURES // BN_CHUNK
            columns = len(group[q]) * PAIR
            if q == group[q].start:
                chunks[q] = small.tile([P, columns, per_tile, 6], F32, name="chunks")
            else:
                chunks[q] = chunks[q - 1]
            for i in range(PAIR):
                for n in range(per_tile):
                    nc.vector.bn_stats(
                        out=chunks[q][:, column(q, i).start, n, :],
                        in_=x_pairs[q][:, i, n * BN_CHUNK : (n + 1) * BN_CHUNK],
                    )
                    if between:
                        between[0]()
                        between.remove(between[0])
            if q == group[q].stop - 1:
                mean_var = small.tile([P, columns, 2], F32)
                for t in range(columns):
                    nc.vector.bn_aggr(
                        out=mean_var[:, t, :], in_=chunks[q][:, t, :, :].rearrange("p n s -> p (n s)")
                    )
                means_sum = small.tile([P, columns], F32)
                nc.vector.tensor_reduce(
                    out=means_sum[:],
                    in_=chunks[q][:].rearrange("p i n (a s) -> p i (n a) s", a=2)[:, :, :, 1],
                    axis=AXIS.X, op=ALU.add,
                )
                var_eps = small.tile([P, columns], F32)
                nc.vector.tensor_scalar(
                    out=var_eps[:], in0=mean_var[:, :, 1], scalar1=EPS, scalar2=None, op0=ALU.add
                )
                nc.vector.tensor_scalar(
                    out=mean[q][:], in0=means_sum[:], scalar1=1.0 / (2 * per_tile), scalar2=None,
                    op0=ALU.mult,
                )
                inverse_std(q, var_eps)

        def scalar_mean(t):
            q, i = t // PAIR, t % PAIR
            unread = stage.tile([P, FEATURES], BF16, name="unread_sum")
            nc.scalar.activation(
                out=unread[:], in_=x_tile(t), func=ACT.Identity, scale=1.0 / FEATURES,
                accum_out=mean[q][:, column(q, i)],
            )

        def scalar_spread(t):
            q, i = t // PAIR, t % PAIR
            unread = stage.tile([P, FEATURES], BF16, name="unread_square")
            if i == 0:
                if q == group[q].start:
                    spreads[q] = small.tile([P, len(group[q]) * PAIR], F32, name="spreads")
                else:
                    spreads[q] = spreads[q - 1]
            nc.scalar.activation(
                out=unread[:], in_=x_tile(t), func=ACT.Square, bias=mean[q][:, column(q, i)],
                scale=-1.0, accum_out=spreads[q][:, column(q, i)],
            )
            if t == group[q].stop * PAIR - 1:
                complete.append(q)

        def finish_spreads():
            for q in complete:
                var_eps = small.tile([P, len(group[q]) * PAIR], F32)
                nc.scalar.activation(
                    out=var_eps[:], in_=spreads[q][:], func=ACT.Identity, bias=eps[:],
                    scale=1.0 / FEATURES,
                )
                inverse_std(q, var_eps)
            complete.clear()

        def tensor_mean(q):
            if q == group[q].start:
                sums[q] = psum_sum.tile(
                    [P, len(group[q]) * PAIR, SUM_COLS], F32, name="sums", tag="sum"
                )
            else:
                sums[q] = sums[q - 1]
            for i in range(PAIR):
                sum_features(sums[q][:, column(q, i).start, :], q * PAIR + i)

        def sum_features(target, t):
            for n in range(FEATURES // SUM_COLS):
                nc.tensor.matmul(
                    out=target, lhsT=ident_mean[:],
                    rhs=x_tile(t)[:, n * SUM_COLS : (n + 1) * SUM_COLS],
                    start=(n == 0), stop=(n == FEATURES // SUM_COLS - 1),
                )

        def tensor_mean_single(t):
            sums[t] = psum_sum.tile([P, SUM_COLS], F32, name="sums1", tag="sum")
            sum_features(sums[t][:], t)

        def finish_mean_single(t):
            q, i = t // PAIR, t % PAIR
            nc.vector.tensor_reduce(
                out=mean[q][:, column(q, i)], in_=sums[t][:], axis=AXIS.X, op=ALU.add
            )

        def finish_mean(q):
            if q == group[q].stop - 1:
                nc.vector.tensor_reduce(out=mean[q][:], in_=sums[q][:], axis=AXIS.X, op=ALU.add)

        def normalise_beside_mix(q):
            i = PAIR - 1
            normed[q] = normed_pool.tile([P, PAIR, FEATURES], BF16, name="normed")
            offset = small.tile([P, 1], F32)
            nc.vector.scalar_tensor_tensor(
                out=offset[:], in0=mean[q][:, column(q, i)], scalar=-1.0,
                in1=rstd[q][:, column(q, i)], op0=ALU.mult, op1=ALU.mult,
            )
            nc.gpsimd.tensor_scalar(
                out=normed[q][:, i, :], in0=x_pairs[q][:, i, :],
                scalar1=rstd[q][:, column(q, i)], scalar2=offset[:], op0=ALU.mult, op1=ALU.add,
            )

        def normalise(q):
            if BESIDE_FIRST <= q < BESIDE_LAST:
                beside = 1
            else:
                beside = 0
                normed[q] = normed_pool.tile([P, PAIR, FEATURES], BF16, name="normed")
            for i in range(PAIR - beside):
                nc.vector.tensor_scalar(
                    out=normed[q][:, i, :], in0=x_pairs[q][:, i, :],
                    scalar1=mean[q][:, column(q, i)], scalar2=rstd[q][:, column(q, i)],
                    op0=ALU.subtract, op1=ALU.mult,
                )

        def transpose(q):
            turned[q] = []
            for i in range(PAIR):
                words = normed[q][:, i, :].bitcast(F32)
                planes = psum_xt.tile([P, PASSES, 2, P], F32)
                for g in range(PASSES):
                    for u in range(2):
                        first = (2 * g + u) * P
                        nc.tensor.transpose(
                            planes[:, g, u, :], words[:, first : first + P], ident_f32[:]
                        )
                turned[q].append(planes)

        def regroup(q):
            grouped[q] = stage.tile([P, PAIR, FEATURES], BF16, name="grouped", align_bytes=64)
            for i in range(PAIR):
                nc.scalar.copy(
                    out=grouped[q][:, i, :].bitcast(F32).rearrange(
                        "p (g r u) -> p g r u", g=PASSES, u=2
                    ),
                    in_=turned[q][i][:].rearrange("p g u r -> p g r u"),
                )

        def quantise(q):
            words = flow.tile([P, PAIR * WORDS], U32, name="a_codes", align_bytes=64)
            plane = flow.tile([P, PAIR * WORDS], U8, name="a_scales", align_bytes=64)
            nc.vector.quantize_mx(
                out=words[:].bitcast(FP8X4), scales=plane[:],
                in_=grouped[q][:].rearrange("p i k -> p (i k)"),
            )
            codes[q] = (words, plane)

        def bias_product(q):
            bias_sums[q] = psum_bias.tile([P, PAIR, HIDDEN], F32, name="bias_sums", tag="bias")
            for i in range(PAIR):
                t = q * PAIR + i
                nc.tensor.matmul(
                    out=bias_sums[q][:, i, :], lhsT=pieces_t[:, t // SLOT_TILES, :],
                    rhs=bias_slot[:, t % SLOT_TILES, :], start=True, stop=True,
                )

        def copy_bias(q):
            bias_mix[q] = flow.tile([P, PAIR, HIDDEN], F32, name="bias_mix")
            nc.scalar.copy(out=bias_mix[q][:], in_=bias_sums[q][:])

        def multiply(q):
            words, plane = codes[q]
            products[q] = [[], []]
            for half in range(HALVES):
                cols = slice(half * N_COLS, (half + 1) * N_COLS)
                for i in range(PAIR):
                    bank = psum_y.tile([P, N_COLS], F32, name="y%d" % half)
                    for g in range(PASSES):
                        rows = slice(i * WORDS + g * P, i * WORDS + (g + 1) * P)
                        nc.tensor.matmul_mx(
                            out=bank[:],
                            lhsT=words[:, rows].bitcast(FP8X4), lhsT_scale=plane[:, rows],
                            rhs=w_codes[:, g, cols].bitcast(FP8X4), rhs_scale=w_scales[:, g, cols],
                            start=(g == 0), stop=(g == PASSES - 1),
                        )
                    products[q][i].append(bank)

        def mix(q):
            mixed[q] = flow.tile([P, PAIR, HIDDEN], F32, name="mixed")
            for x in range(EXPERTS):
                for i in range(PAIR):
                    t = q * PAIR + i
                    bank = products[q][i][x * HIDDEN // N_COLS]
                    first = x * HIDDEN % N_COLS
                    nc.vector.scalar_tensor_tensor(
                        out=mixed[q][:, i, :], in0=bank[:, first : first + HIDDEN],
                        scalar=coeff[:, t, x : x + 1],
                        in1=(bias_mix[q] if x == 0 else mixed[q])[:, i, :],
                        op0=ALU.mult, op1=ALU.add,
                    )

        def exponential(q):
            mixed_exp[q] = flow.tile([P, PAIR, HIDDEN], F32, name="mixed_exp")
            nc.scalar.activation(out=mixed_exp[q][:], in_=mixed[q][:], func=ACT.Exp)

        def relu(q):
            below[q] = flow.tile([P, PAIR, HIDDEN], F32, name="below")
            nc.scalar.activation(out=below[q][:], in_=mixed[q][:], func=ACT.Relu)

        def relu_and_store(q):
            result = flow.tile([P, PAIR, HIDDEN], F32)
            nc.vector.scalar_tensor_tensor(
                out=result[:], in0=mixed_exp[q][:], scalar=1.0, in1=below[q][:],
                op0=ALU.subtract, op1=ALU.min,
            )
            nc.sync.dma_start(out=out_rows[:, q * PAIR : (q + 1) * PAIR, :], in_=result[:])

        def elu_beside_vector(q):
            lack = flow.tile([P, PAIR, HIDDEN], F32)
            nc.scalar.activation(
                out=lack[:], in_=mixed_exp[q][:], func=ACT.Relu, bias=one[:], scale=-1.0
            )
            result = flow.tile([P, PAIR, HIDDEN], F32, name="result_beside")
            nc.gpsimd.tensor_tensor(
                out=result[:], in0=below[q][:], in1=lack[:], op=ALU.subtract
            )
            nc.sync.dma_start(out=out_rows[:, q * PAIR : (q + 1) * PAIR, :], in_=result[:])

        def last_elu_and_store(q):
            ramp = flow.tile([P, PAIR, HIDDEN], F32)
            nc.vector.tensor_scalar(
                out=ramp[:], in0=mixed[q][:], scalar1=0.0, scalar2=None, op0=ALU.max
            )
            for i in range(PAIR):
                power = flow.tile([P, HIDDEN], F32, name="power%d" % i)
                nc.scalar.activation(out=power[:], in_=mixed[q][:, i, :], func=ACT.Exp)
                result = flow.tile([P, HIDDEN], F32, name="result%d" % i)
                nc.vector.scalar_tensor_tensor(
                    out=result[:], in0=power[:], scalar=1.0, in1=ramp[:, i, :],
                    op0=ALU.subtract, op1=ALU.min,
                )
                nc.sync.dma_start(out=out_rows[:, q * PAIR + i, :], in_=result[:])

        def below_zero(q):
            below[q] = flow.tile([P, PAIR, HIDDEN], F32, name="below")
            nc.vector.tensor_scalar(
                out=below[q][:], in0=mixed_exp[q][:], scalar1=1.0, scalar2=-1.0,
                op0=ALU.min, op1=ALU.add,
            )

        def elu_and_store(q):
            result = flow.tile([P, PAIR, HIDDEN], F32)
            nc.vector.tensor_tensor(out=result[:], in0=mixed[q][:], in1=below[q][:], op=ALU.max)
            nc.sync.dma_start(out=out_rows[:, q * PAIR : (q + 1) * PAIR, :], in_=result[:])

        def run(stage_of_pair, q, first=0, last=PAIRS):
            if first <= q < last:
                stage_of_pair(q)

        def two_pass_tiles(first, last):
            passes = []
            for t in range(first, last + 1):
                if t < last:
                    passes.append((scalar_mean, t))
                if t > first:
                    passes.append((scalar_spread, t - 1))
            return passes

        passes = two_pass_tiles(HEAD_PAIRS * PAIR, SUMMED_FIRST * PAIR)
        for t in range(SUMMED_LAST * PAIR + 1, TILES):
            passes.append((scalar_mean, t))
        for t in range(SUMMED_FIRST * PAIR, TILES):
            passes.append((scalar_spread, t))

        def scalar_stats(count):
            for taken in range(min(count, len(passes))):
                stage_of_tile, t = passes[0]
                passes.remove(passes[0])
                stage_of_tile(t)

        for s in range(-4, PAIRS + 1):
            run(exponential, s - 1, last=PAIRS - 1)
            run(relu, s - 1, 9, PAIRS - 1)
            run(elu_beside_vector, s - 1, 13, PAIRS - 1)
            if s == -2:
                for step in coefficient_steps:
                    step()
                transpose_pieces()
            run(normalise, s + 2)
            run(transpose, s + 2)
            if s == -2:
                regroup_weights()
            if s == -1:
                quantise_weights()
            run(quantise, s + 1)
            if s == -2:
                copy_pieces()
            run(bias_product, s + 2)
            run(below_zero, s - 2, last=9)
            run(normalise_beside_mix, s + 3, BESIDE_FIRST, BESIDE_LAST)
            run(mix, s)
            run(multiply, s + 1)
            run(finish_mean, s + 8, SUMMED_FIRST, SUMMED_LAST)
            if s == -2:
                tensor_mean(SUMMED_FIRST)
            run(tensor_mean, s + 9, SUMMED_FIRST + 1, SUMMED_LAST)
            if s == 5:
                tensor_mean_single(SUMMED_LAST * PAIR)
            if s == 6:
                finish_mean_single(SUMMED_LAST * PAIR)
            run(elu_and_store, s - 2, last=9)
            run(relu_and_store, s - 2, 9, 13)
            if s + 4 < HEAD_PAIRS:
                vector_stats(s + 4, coefficient_steps if s < -2 else [])
            if s > -4:
                scalar_stats(1)
            run(regroup, s + 2)
            finish_spreads()
            scalar_stats(4 if s == -4 else 2 if s == -1 else 1)
            run(copy_bias, s + 2)
            finish_spreads()
            run(last_elu_and_store, s - 1, PAIRS - 1)
